import numpy as np
import ml_dtypes


def mxq(x, axis, fmt="e4m3"):
    dtype, down = {"e4m3": (ml_dtypes.float8_e4m3fn, 7), "e5m2": (ml_dtypes.float8_e5m2, 14)}[fmt]
    v = np.moveaxis(np.asarray(x, np.float32).astype(ml_dtypes.bfloat16).astype(np.float64), axis, -1)
    blocks = v.reshape(v.shape[:-1] + (-1, 32))
    amax = np.abs(blocks).max(-1, keepdims=True)
    byte = np.maximum(np.where(amax > 0, np.frexp(amax)[1] - 1 + 127, 0) - down, 1)
    scale = np.exp2(byte - 127.0)
    codes = (blocks / scale).astype(np.float32).astype(dtype).astype(np.float64)
    return np.moveaxis((codes * scale).reshape(v.shape), -1, axis)


WIDE = False


def mx_kscale(k):
    if not WIDE:
        return np.ones(k)
    levels = np.array([10, -10, 5, -5, 0])
    a = np.random.permutation(np.resize(levels, k // 512 * 4)).reshape(k // 512, 4)
    idx = np.arange(k)
    return np.exp2(a[idx // 512, idx % 128 // 32])


BF16 = ml_dtypes.bfloat16


def bf(x):
    return np.asarray(x, np.float32).astype(BF16)


def f64(x):
    return np.asarray(x).astype(np.float64)


B, S, FIN, D, AF, F, H = 4, 1024, 128, 512, 2048, 1024, 16
EPS = 1e-3


def layer_norm(v, gamma, beta):
    mu = v.mean(-1, keepdims=True)
    var = v.var(-1, keepdims=True)
    return (v - mu) / np.sqrt(var + EPS) * gamma + beta


def setup_inputs():
    r = np.random.standard_normal
    t = mx_kscale(F)
    return {"h_attn": bf(r((B, S, D))),
            "W1": bf(r((D, F)) / np.sqrt(D) * t), "b1": bf(0.1 * r(F) * t),
            "W2": bf(r((F, D)) / np.sqrt(F) / t[:, None]), "b2": bf(0.1 * r(D)),
            "g2": bf(1.0 + 0.1 * r(D)), "beta2": bf(0.1 * r(D))}


def reference(h_attn, W1, b1, W2, b2, g2, beta2):
    h = f64(h_attn)
    hid = np.maximum((mxq(h, 2, "e4m3") @ mxq(f64(W1), 0, "e4m3")) + f64(b1), 0.0)
    ffn = (mxq(hid, 2, "e4m3") @ mxq(f64(W2), 0, "e4m3")) + f64(b2)
    return layer_norm(h + ffn, f64(g2), f64(beta2))

@@ -1,0 +1,254 @@
+from contextlib import ExitStack
+
+import concourse.bass as bass
+import concourse.mybir as mybir
+import concourse.tile as tile
+from concourse.masks import make_identity
+
+F32 = mybir.dt.float32
+BF16 = mybir.dt.bfloat16
+U32 = mybir.dt.uint32
+U8 = mybir.dt.uint8
+FP8X4 = mybir.dt.float8_e4m3fn_x4
+ALU = mybir.AluOpType
+ACT = mybir.ActivationFunctionType
+
+P = 128
+T = 4096
+D = 512
+F = 1024
+GT = 512
+NG = T // GT
+EPS = 1e-3
+FLOPS = 2 * T * D * F * 2
+
+
+def tile_ffnn_encoder_pc_t_kernel(tc, h_attn, W1, b1, W2, b2, g2, beta2, out):
+    nc = tc.nc
+    h = h_attn.flatten_outer_dims()
+    o = out.flatten_outer_dims()
+    with ExitStack() as ctx:
+        keep = ctx.enter_context(tc.tile_pool(name="keep", bufs=1))
+        work = ctx.enter_context(tc.tile_pool(name="work", bufs=2))
+        ps_const = ctx.enter_context(tc.psum_pool(name="ps_const", bufs=1))
+        ps_a = ctx.enter_context(tc.psum_pool(name="ps_a", bufs=2))
+        ps_b = ctx.enter_context(tc.psum_pool(name="ps_b", bufs=3))
+        ps_c = ctx.enter_context(tc.psum_pool(name="ps_c", bufs=2))
+
+        eps_t = keep.tile([P, 1], F32)
+        nc.vector.memset(eps_t[:], EPS)
+        scr = keep.tile([P, 1], F32)
+        nc.scalar.activation(out=scr[:], in_=eps_t[:], func=ACT.Sqrt)
+        ones = keep.tile([P, P], BF16)
+        nc.vector.memset(ones[:], 1.0)
+        rowz = keep.tile([P, 3 * D], BF16)
+        nc.vector.memset(rowz[:], 0.0)
+        ident = keep.tile([P, P], F32)
+        make_identity(nc, ident[:])
+
+        b1raw = keep.tile([P, 2, 4], BF16)
+        nc.scalar.dma_start(out=b1raw[:], in_=b1.rearrange("(g p t) -> p g t", g=2, t=4))
+        nc.scalar.dma_start(out=rowz[0:1, 0:D], in_=g2.rearrange("(o d) -> o d", o=1))
+        nc.scalar.dma_start(out=rowz[0:1, D:2 * D], in_=beta2.rearrange("(o d) -> o d", o=1))
+        nc.scalar.dma_start(out=rowz[0:1, 2 * D:3 * D], in_=b2.rearrange("(o d) -> o d", o=1))
+
+        w1raw = keep.tile([P, 4, F], BF16)
+        w2raw = keep.tile([P, 2, 4, D], BF16)
+        h_sb = [keep.tile([P, 4 * D], BF16, name="h%d" % g) for g in range(NG)]
+
+        def load_h(g):
+            nc.sync.dma_start(
+                out=h_sb[g][:],
+                in_=h[g * GT:(g + 1) * GT, :].rearrange("(p j) d -> p (j d)", j=4),
+            )
+
+        def load_w1(gg):
+            for u in range(2):
+                nc.sync.dma_start(
+                    out=w1raw[:, 2 * u:2 * u + 2, gg * 512:(gg + 1) * 512],
+                    in_=W1[256 * u:256 * u + 256, gg * 512:(gg + 1) * 512].rearrange(
+                        "(q e) f -> q e f", e=2
+                    ),
+                )
+
+        load_w1(0)
+        load_h(0)
+        load_w1(1)
+        for gg in range(2):
+            nc.sync.dma_start(
+                out=w2raw[:, gg],
+                in_=W2[512 * gg:512 * gg + 512, :].rearrange("(p t) d -> p t d", t=4),
+            )
+        for g in range(1, NG):
+            load_h(g)
+
+        b1f = keep.tile([P, 8], F32)
+        nc.vector.tensor_copy(out=b1f[:], in_=b1raw[:].rearrange("p g t -> p (g t)"))
+
+        w1g = keep.tile([P, 4 * F], BF16, align_bytes=64)
+        w1c = keep.tile([P, F], U32, align_bytes=64)
+        w1s = keep.tile([P, F], U8, align_bytes=64)
+        w2g = keep.tile([P, 2 * 4 * D], BF16, align_bytes=64)
+        w2c = keep.tile([P, 2 * D], U32, align_bytes=64)
+        w2s = keep.tile([P, 2 * D], U8, align_bytes=64)
+        for gg in range(2):
+            src = w1raw[:, :, gg * 512:(gg + 1) * 512].rearrange("q t (p s) -> q s p t", s=4)
+            dst = w1g[:, gg * 2048:(gg + 1) * 2048].rearrange("q (s p t) -> q s p t", s=4, t=4)
+            if gg == 0:
+                nc.vector.tensor_copy(out=dst, in_=src)
+            else:
+                nc.scalar.copy(out=dst, in_=src)
+        for gg in range(2):
+            nc.vector.quantize_mx(
+                out=w1c[:, gg * 512:(gg + 1) * 512].bitcast(FP8X4),
+                scales=w1s[:, gg * 512:(gg + 1) * 512],
+                in_=w1g[:, gg * 2048:(gg + 1) * 2048],
+            )
+
+        cst = ps_const.tile([P, 2 * D], BF16)
+        nc.tensor.matmul(out=cst[:, 0:D], lhsT=ones[:], rhs=rowz[:, 0:D], start=True, stop=True)
+        nc.tensor.matmul(out=cst[:, D:2 * D], lhsT=ones[:], rhs=rowz[:, D:2 * D], start=True, stop=True)
+        b2ps = ps_c.tile([P, D], F32, tag="fo")
+        nc.tensor.matmul(out=b2ps[:], lhsT=ones[:], rhs=rowz[:, 2 * D:3 * D], start=True, stop=True)
+        b2bc = keep.tile([P, D], F32)
+        nc.vector.tensor_copy(out=b2bc[:], in_=b2ps[:])
+
+        state = {}
+
+        def stage_a(g):
+            hw = h_sb[g][:].bitcast(F32)
+            hg = work.tile([P, 4 * GT], BF16, align_bytes=64, tag="hg")
+            hgw = hg[:].bitcast(F32).rearrange("q (c u) -> q c u", u=2)
+            for jj in range(2):
+                xt = ps_a.tile([P, 512], F32, tag="xt")
+                for jl in range(2):
+                    j = 2 * jj + jl
+                    for u in range(2):
+                        nc.tensor.transpose(
+                            xt[:, u * 256 + jl * 128:u * 256 + jl * 128 + 128],
+                            hw[:, j * 256 + u * 128:j * 256 + u * 128 + 128],
+                            ident[:],
+                        )
+                nc.scalar.copy(
+                    out=hgw[:, jj * 256:(jj + 1) * 256, :],
+                    in_=xt[:].rearrange("q (u c) -> q c u", u=2),
+                )
+            hc = work.tile([P, GT], U32, align_bytes=64, tag="hc", bufs=3)
+            hs = work.tile([P, GT], U8, align_bytes=64, tag="hs", bufs=3)
+            nc.vector.quantize_mx(out=hc[:].bitcast(FP8X4), scales=hs[:], in_=hg[:])
+            hb = work.tile([P, 4, D], F32, tag="hb", bufs=3)
+            nc.gpsimd.tensor_tensor(
+                out=hb[:],
+                in0=h_sb[g][:].rearrange("p (j d) -> p j d", j=4),
+                in1=b2bc[:].unsqueeze(1).to_broadcast([P, 4, D]),
+                op=ALU.add,
+            )
+            state[("a", g)] = (hc, hs, hb)
+
+        def stage_b(g):
+            hc, hs, hb = state[("a", g)]
+            res = []
+            for gg in range(2):
+                hid_p = work.tile([P, 4, GT], BF16, tag="hid_p", bufs=3)
+                for s in range(4):
+                    b = 4 * gg + s
+                    hp = ps_b.tile([P, GT], F32, tag="hp")
+                    nc.tensor.matmul_mx(
+                        out=hp[:],
+                        lhsT=w1c[:, b * 128:(b + 1) * 128].bitcast(FP8X4),
+                        lhsT_scale=w1s[:, b * 128:(b + 1) * 128],
+                        rhs=hc[:].bitcast(FP8X4),
+                        rhs_scale=hs[:],
+                        start=True,
+                        stop=True,
+                    )
+                    nc.scalar.activation(
+                        out=hid_p[:, s, :], in_=hp[:], func=ACT.Relu, bias=b1f[:, b:b + 1], scale=1.0
+                    )
+                hid_g = work.tile([P, 4 * GT], BF16, align_bytes=64, tag="hid_g", bufs=3)
+                nc.vector.tensor_copy(
+                    out=hid_g[:].rearrange("p (c i t) -> p c t i", i=4, t=4),
+                    in_=hid_p[:].rearrange("p t (c i) -> p c t i", i=4),
+                )
+                res.append(hid_g)
+            codes = []
+            for gg in range(2):
+                hid_c = work.tile([P, GT], U32, align_bytes=64, tag="hid_c", bufs=4)
+                hid_s = work.tile([P, GT], U8, align_bytes=64, tag="hid_s", bufs=4)
+                nc.vector.quantize_mx(out=hid_c[:].bitcast(FP8X4), scales=hid_s[:], in_=res[gg][:])
+                codes.append((hid_c, hid_s))
+            state[("b", g)] = codes
+
+        def stage_c(g):
+            hc, hs, hb = state[("a", g)]
+            codes = state[("b", g)]
+            s1 = work.tile([P, 4], F32, tag="s1", bufs=3)
+            s2 = work.tile([P, 4], F32, tag="s2", bufs=3)
+            negmu = work.tile([P, 4], F32, tag="negmu", bufs=3)
+            std = work.tile([P, 4], F32, tag="std", bufs=3)
+            rstd = work.tile([P, 4], F32, tag="rstd", bufs=3)
+            ot = work.tile([P, 4 * D], F32, tag="ot", bufs=2)
+            rs = []
+            for j in range(4):
+                fo = ps_c.tile([P, D], F32, tag="fo")
+                for gg in range(2):
+                    hid_c, hid_s = codes[gg]
+                    nc.tensor.matmul_mx(
+                        out=fo[:],
+                        lhsT=hid_c[:, j * 128:(j + 1) * 128].bitcast(FP8X4),
+                        lhsT_scale=hid_s[:, j * 128:(j + 1) * 128],
+                        rhs=w2c[:, gg * D:(gg + 1) * D].bitcast(FP8X4),
+                        rhs_scale=w2s[:, gg * D:(gg + 1) * D],
+                        start=(gg == 0),
+                        stop=(gg == 1),
+                    )
+                r = work.tile([P, D], F32, tag="r", bufs=8)
+                nc.vector.scalar_tensor_tensor(
+                    out=r[:], in0=fo[:], scalar=0.0, in1=hb[:, j, :], op0=ALU.add, op1=ALU.add,
+                    accum_out=s1[:, j:j + 1],
+                )
+                rs.append(r)
+            nc.vector.tensor_scalar(
+                out=negmu[:], in0=s1[:], scalar1=-1.0 / D, scalar2=None, op0=ALU.mult
+            )
+            for j in range(4):
+                junk = work.tile([P, D], BF16, tag="junk", bufs=2)
+                nc.scalar.activation(
+                    out=junk[:], in_=rs[j][:], func=ACT.Square, bias=negmu[:, j:j + 1], scale=1.0,
+                    accum_out=s2[:, j:j + 1],
+                )
+            nc.scalar.activation(out=std[:], in_=s2[:], func=ACT.Sqrt, bias=eps_t[:, 0:1], scale=1.0 / D)
+            nc.vector.reciprocal(out=rstd[:], in_=std[:])
+            for j in range(4):
+                t1 = work.tile([P, D], F32, tag="t1", bufs=4)
+                nc.vector.scalar_tensor_tensor(
+                    out=t1[:], in0=rs[j][:], scalar=negmu[:, j:j + 1], in1=cst[:, 0:D],
+                    op0=ALU.add, op1=ALU.mult,
+                )
+                nc.vector.scalar_tensor_tensor(
+                    out=ot[:, j * D:(j + 1) * D], in0=t1[:], scalar=rstd[:, j:j + 1], in1=cst[:, D:2 * D],
+                    op0=ALU.mult, op1=ALU.add,
+                )
+            nc.sync.dma_start(
+                out=o[g * GT:(g + 1) * GT, :].rearrange("(p j) d -> p (j d)", j=4), in_=ot[:]
+            )
+
+        stage_a(0)
+        for gg in range(2):
+            nc.vector.tensor_copy(
+                out=w2g[:, gg * 2048:(gg + 1) * 2048].rearrange("p (c i t) -> p c t i", i=4, t=4),
+                in_=w2raw[:, gg].rearrange("p t (c i) -> p c t i", i=4),
+            )
+        for gg in range(2):
+            nc.vector.quantize_mx(
+                out=w2c[:, gg * D:(gg + 1) * D].bitcast(FP8X4),
+                scales=w2s[:, gg * D:(gg + 1) * D],
+                in_=w2g[:, gg * 2048:(gg + 1) * 2048],
+            )
+        for step in range(1, NG + 2):
+            if step < NG:
+                stage_a(step)
+            if 1 <= step <= NG:
+                stage_b(step - 1)
+            if step >= 2:
+                stage_c(step - 2)

@@ -32,7 +32,7 @@ def tile_ffnn_encoder_pc_t_kernel(tc, h_attn, W1, b1, W2, b2, g2, beta2, out):
         work = ctx.enter_context(tc.tile_pool(name="work", bufs=2))
         ps_const = ctx.enter_context(tc.psum_pool(name="ps_const", bufs=1))
         ps_a = ctx.enter_context(tc.psum_pool(name="ps_a", bufs=2))
-        ps_b = ctx.enter_context(tc.psum_pool(name="ps_b", bufs=3))
+        ps_b = ctx.enter_context(tc.psum_pool(name="ps_b", bufs=2))
         ps_c = ctx.enter_context(tc.psum_pool(name="ps_c", bufs=2))
 
         eps_t = keep.tile([P, 1], F32)
@@ -108,10 +108,8 @@ def tile_ffnn_encoder_pc_t_kernel(tc, h_attn, W1, b1, W2, b2, g2, beta2, out):
         cst = ps_const.tile([P, 2 * D], BF16)
         nc.tensor.matmul(out=cst[:, 0:D], lhsT=ones[:], rhs=rowz[:, 0:D], start=True, stop=True)
         nc.tensor.matmul(out=cst[:, D:2 * D], lhsT=ones[:], rhs=rowz[:, D:2 * D], start=True, stop=True)
-        b2ps = ps_c.tile([P, D], F32, tag="fo")
-        nc.tensor.matmul(out=b2ps[:], lhsT=ones[:], rhs=rowz[:, 2 * D:3 * D], start=True, stop=True)
-        b2bc = keep.tile([P, D], F32)
-        nc.vector.tensor_copy(out=b2bc[:], in_=b2ps[:])
+        cst2 = ps_const.tile([P, D], BF16)
+        nc.tensor.matmul(out=cst2[:], lhsT=ones[:], rhs=rowz[:, 2 * D:3 * D], start=True, stop=True)
 
         state = {}
 
@@ -137,10 +135,10 @@ def tile_ffnn_encoder_pc_t_kernel(tc, h_attn, W1, b1, W2, b2, g2, beta2, out):
             hs = work.tile([P, GT], U8, align_bytes=64, tag="hs", bufs=3)
             nc.vector.quantize_mx(out=hc[:].bitcast(FP8X4), scales=hs[:], in_=hg[:])
             hb = work.tile([P, 4, D], F32, tag="hb", bufs=3)
-            nc.gpsimd.tensor_tensor(
+            nc.vector.tensor_tensor(
                 out=hb[:],
                 in0=h_sb[g][:].rearrange("p (j d) -> p j d", j=4),
-                in1=b2bc[:].unsqueeze(1).to_broadcast([P, 4, D]),
+                in1=cst2[:].unsqueeze(1).to_broadcast([P, 4, D]),
                 op=ALU.add,
             )
             state[("a", g)] = (hc, hs, hb)
@@ -166,10 +164,16 @@ def tile_ffnn_encoder_pc_t_kernel(tc, h_attn, W1, b1, W2, b2, g2, beta2, out):
                         out=hid_p[:, s, :], in_=hp[:], func=ACT.Relu, bias=b1f[:, b:b + 1], scale=1.0
                     )
                 hid_g = work.tile([P, 4 * GT], BF16, align_bytes=64, tag="hid_g", bufs=3)
-                nc.vector.tensor_copy(
-                    out=hid_g[:].rearrange("p (c i t) -> p c t i", i=4, t=4),
-                    in_=hid_p[:].rearrange("p t (c i) -> p c t i", i=4),
-                )
+                if gg == 1 or g % 2 == 1:
+                    nc.scalar.copy(
+                        out=hid_g[:].rearrange("p (c i t) -> p c t i", i=4, t=4),
+                        in_=hid_p[:].rearrange("p t (c i) -> p c t i", i=4),
+                    )
+                else:
+                    nc.vector.tensor_copy(
+                        out=hid_g[:].rearrange("p (c i t) -> p c t i", i=4, t=4),
+                        in_=hid_p[:].rearrange("p t (c i) -> p c t i", i=4),
+                    )
                 res.append(hid_g)
             codes = []
             for gg in range(2):
@@ -235,7 +239,7 @@ def tile_ffnn_encoder_pc_t_kernel(tc, h_attn, W1, b1, W2, b2, g2, beta2, out):
 
         stage_a(0)
         for gg in range(2):
-            nc.vector.tensor_copy(
+            nc.scalar.copy(
                 out=w2g[:, gg * 2048:(gg + 1) * 2048].rearrange("p (c i t) -> p c t i", i=4, t=4),
                 in_=w2raw[:, gg].rearrange("p t (c i) -> p c t i", i=4),
             )

@@ -1,8 +1,6 @@
 from contextlib import ExitStack
 
-import concourse.bass as bass
 import concourse.mybir as mybir
-import concourse.tile as tile
 from concourse.masks import make_identity
 
 F32 = mybir.dt.float32
@@ -14,13 +12,16 @@ ALU = mybir.AluOpType
 ACT = mybir.ActivationFunctionType
 
 P = 128
-T = 4096
+TOKENS = 4096
 D = 512
 F = 1024
-GT = 512
-NG = T // GT
 EPS = 1e-3
-FLOPS = 2 * T * D * F * 2
+FLOPS = 2 * TOKENS * D * F * 2
+
+GROUP = 512
+TILES = GROUP // P
+GROUPS = TOKENS // GROUP
+BANK = 512
 
 
 def tile_ffnn_encoder_pc_t_kernel(tc, h_attn, W1, b1, W2, b2, g2, beta2, out):
@@ -30,60 +31,82 @@ def tile_ffnn_encoder_pc_t_kernel(tc, h_attn, W1, b1, W2, b2, g2, beta2, out):
     with ExitStack() as ctx:
         keep = ctx.enter_context(tc.tile_pool(name="keep", bufs=1))
         work = ctx.enter_context(tc.tile_pool(name="work", bufs=2))
-        ps_const = ctx.enter_context(tc.psum_pool(name="ps_const", bufs=1))
-        ps_a = ctx.enter_context(tc.psum_pool(name="ps_a", bufs=2))
-        ps_b = ctx.enter_context(tc.psum_pool(name="ps_b", bufs=2))
-        ps_c = ctx.enter_context(tc.psum_pool(name="ps_c", bufs=2))
+        psum = ctx.enter_context(tc.psum_pool(name="psum", bufs=1))
+        ctx.enter_context(tc.manual_schedule())
+
+        ring_size = {"s": 5, "v": 2}
+        ring_next = {"s": 0, "v": 0}
+
+        def next_bank(ring, dtype=F32, cols=BANK):
+            k = ring_next[ring] % ring_size[ring]
+            ring_next[ring] += 1
+            return psum.tile([P, cols], dtype, tag="%s%d" % (ring, k), name="%s%d" % (ring, k))
 
         eps_t = keep.tile([P, 1], F32)
         nc.vector.memset(eps_t[:], EPS)
-        scr = keep.tile([P, 1], F32)
-        nc.scalar.activation(out=scr[:], in_=eps_t[:], func=ACT.Sqrt)
+        warm = keep.tile([P, 1], F32)
+        nc.scalar.activation(out=warm[:], in_=eps_t[:], func=ACT.Sqrt)
         ones = keep.tile([P, P], BF16)
         nc.vector.memset(ones[:], 1.0)
-        rowz = keep.tile([P, 3 * D], BF16)
-        nc.vector.memset(rowz[:], 0.0)
+        rows = keep.tile([P, 2 * D], BF16)
+        nc.vector.memset(rows[:], 0.0)
+        b2rows = keep.tile([P, P], BF16)
+        nc.vector.memset(b2rows[:], 0.0)
         ident = keep.tile([P, P], F32)
         make_identity(nc, ident[:])
+        identb = keep.tile([P, P], BF16)
+        make_identity(nc, identb[:])
 
         b1raw = keep.tile([P, 2, 4], BF16)
         nc.scalar.dma_start(out=b1raw[:], in_=b1.rearrange("(g p t) -> p g t", g=2, t=4))
-        nc.scalar.dma_start(out=rowz[0:1, 0:D], in_=g2.rearrange("(o d) -> o d", o=1))
-        nc.scalar.dma_start(out=rowz[0:1, D:2 * D], in_=beta2.rearrange("(o d) -> o d", o=1))
-        nc.scalar.dma_start(out=rowz[0:1, 2 * D:3 * D], in_=b2.rearrange("(o d) -> o d", o=1))
+        nc.scalar.dma_start(out=rows[0:1, 0:D], in_=g2.rearrange("(o d) -> o d", o=1))
+        nc.scalar.dma_start(out=rows[0:1, D:2 * D], in_=beta2.rearrange("(o d) -> o d", o=1))
+        nc.scalar.dma_start(out=b2rows[0:4, :], in_=b2.rearrange("(b p) -> b p", b=4))
 
+        h_sb = [keep.tile([P, TILES * D], BF16, name="h%d" % g) for g in range(GROUPS)]
         w1raw = keep.tile([P, 4, F], BF16)
         w2raw = keep.tile([P, 2, 4, D], BF16)
-        h_sb = [keep.tile([P, 4 * D], BF16, name="h%d" % g) for g in range(NG)]
 
         def load_h(g):
             nc.sync.dma_start(
                 out=h_sb[g][:],
-                in_=h[g * GT:(g + 1) * GT, :].rearrange("(p j) d -> p (j d)", j=4),
+                in_=h[g * GROUP:(g + 1) * GROUP, :].rearrange("(p j) d -> p (j d)", j=TILES),
             )
 
-        def load_w1(gg):
+        def load_w1(half):
             for u in range(2):
                 nc.sync.dma_start(
-                    out=w1raw[:, 2 * u:2 * u + 2, gg * 512:(gg + 1) * 512],
-                    in_=W1[256 * u:256 * u + 256, gg * 512:(gg + 1) * 512].rearrange(
+                    out=w1raw[:, 2 * u:2 * u + 2, half * 512:(half + 1) * 512],
+                    in_=W1[256 * u:256 * u + 256, half * 512:(half + 1) * 512].rearrange(
                         "(q e) f -> q e f", e=2
                     ),
                 )
 
-        load_w1(0)
         load_h(0)
+        load_w1(0)
         load_w1(1)
-        for gg in range(2):
+        load_h(1)
+        for half in range(2):
             nc.sync.dma_start(
-                out=w2raw[:, gg],
-                in_=W2[512 * gg:512 * gg + 512, :].rearrange("(p t) d -> p t d", t=4),
+                out=w2raw[:, half],
+                in_=W2[512 * half:512 * half + 512, :].rearrange("(p t) d -> p t d", t=4),
             )
-        for g in range(1, NG):
+        for g in range(2, GROUPS):
             load_h(g)
 
         b1f = keep.tile([P, 8], F32)
         nc.vector.tensor_copy(out=b1f[:], in_=b1raw[:].rearrange("p g t -> p (g t)"))
+
+        beta2_bc = psum.tile([P, D], BF16, tag="beta2", name="beta2_bc")
+        nc.tensor.matmul(out=beta2_bc[:], lhsT=ones[:], rhs=rows[:, D:2 * D], start=True, stop=True)
+        g2_ps = next_bank("s")
+        nc.tensor.matmul(out=g2_ps[:], lhsT=ones[:], rhs=rows[:, 0:D], start=True, stop=True)
+        g2_bc = keep.tile([P, D], F32)
+        nc.vector.tensor_copy(out=g2_bc[:], in_=g2_ps[:])
+        b2_ps = next_bank("s", BF16, P)
+        nc.tensor.transpose(b2_ps[:], b2rows[:], identb[:])
+        b2f = keep.tile([P, 4], F32)
+        nc.vector.tensor_copy(out=b2f[:], in_=b2_ps[:, 0:4])
 
         w1g = keep.tile([P, 4 * F], BF16, align_bytes=64)
         w1c = keep.tile([P, F], U32, align_bytes=64)
@@ -91,168 +114,261 @@ def tile_ffnn_encoder_pc_t_kernel(tc, h_attn, W1, b1, W2, b2, g2, beta2, out):
         w2g = keep.tile([P, 2 * 4 * D], BF16, align_bytes=64)
         w2c = keep.tile([P, 2 * D], U32, align_bytes=64)
         w2s = keep.tile([P, 2 * D], U8, align_bytes=64)
-        for gg in range(2):
-            src = w1raw[:, :, gg * 512:(gg + 1) * 512].rearrange("q t (p s) -> q s p t", s=4)
-            dst = w1g[:, gg * 2048:(gg + 1) * 2048].rearrange("q (s p t) -> q s p t", s=4, t=4)
-            if gg == 0:
-                nc.vector.tensor_copy(out=dst, in_=src)
-            else:
-                nc.scalar.copy(out=dst, in_=src)
-        for gg in range(2):
+
+        def regroup_w1(half, copy):
+            copy(
+                out=w1g[:, half * 2048:(half + 1) * 2048].rearrange("q (s p t) -> q s p t", s=4, t=4),
+                in_=w1raw[:, :, half * 512:(half + 1) * 512].rearrange("q t (p s) -> q s p t", s=4),
+            )
+
+        def quantise_w1(half):
             nc.vector.quantize_mx(
-                out=w1c[:, gg * 512:(gg + 1) * 512].bitcast(FP8X4),
-                scales=w1s[:, gg * 512:(gg + 1) * 512],
-                in_=w1g[:, gg * 2048:(gg + 1) * 2048],
+                out=w1c[:, half * 512:(half + 1) * 512].bitcast(FP8X4),
+                scales=w1s[:, half * 512:(half + 1) * 512],
+                in_=w1g[:, half * 2048:(half + 1) * 2048],
             )
 
-        cst = ps_const.tile([P, 2 * D], BF16)
-        nc.tensor.matmul(out=cst[:, 0:D], lhsT=ones[:], rhs=rowz[:, 0:D], start=True, stop=True)
-        nc.tensor.matmul(out=cst[:, D:2 * D], lhsT=ones[:], rhs=rowz[:, D:2 * D], start=True, stop=True)
-        cst2 = ps_const.tile([P, D], BF16)
-        nc.tensor.matmul(out=cst2[:], lhsT=ones[:], rhs=rowz[:, 2 * D:3 * D], start=True, stop=True)
-
-        state = {}
-
-        def stage_a(g):
-            hw = h_sb[g][:].bitcast(F32)
-            hg = work.tile([P, 4 * GT], BF16, align_bytes=64, tag="hg")
-            hgw = hg[:].bitcast(F32).rearrange("q (c u) -> q c u", u=2)
-            for jj in range(2):
-                xt = ps_a.tile([P, 512], F32, tag="xt")
-                for jl in range(2):
-                    j = 2 * jj + jl
-                    for u in range(2):
-                        nc.tensor.transpose(
-                            xt[:, u * 256 + jl * 128:u * 256 + jl * 128 + 128],
-                            hw[:, j * 256 + u * 128:j * 256 + u * 128 + 128],
-                            ident[:],
-                        )
-                nc.scalar.copy(
-                    out=hgw[:, jj * 256:(jj + 1) * 256, :],
-                    in_=xt[:].rearrange("q (u c) -> q c u", u=2),
-                )
-            hc = work.tile([P, GT], U32, align_bytes=64, tag="hc", bufs=3)
-            hs = work.tile([P, GT], U8, align_bytes=64, tag="hs", bufs=3)
-            nc.vector.quantize_mx(out=hc[:].bitcast(FP8X4), scales=hs[:], in_=hg[:])
-            hb = work.tile([P, 4, D], F32, tag="hb", bufs=3)
-            nc.vector.tensor_tensor(
-                out=hb[:],
-                in0=h_sb[g][:].rearrange("p (j d) -> p j d", j=4),
-                in1=cst2[:].unsqueeze(1).to_broadcast([P, 4, D]),
-                op=ALU.add,
-            )
-            state[("a", g)] = (hc, hs, hb)
-
-        def stage_b(g):
-            hc, hs, hb = state[("a", g)]
-            res = []
-            for gg in range(2):
-                hid_p = work.tile([P, 4, GT], BF16, tag="hid_p", bufs=3)
-                for s in range(4):
-                    b = 4 * gg + s
-                    hp = ps_b.tile([P, GT], F32, tag="hp")
-                    nc.tensor.matmul_mx(
-                        out=hp[:],
-                        lhsT=w1c[:, b * 128:(b + 1) * 128].bitcast(FP8X4),
-                        lhsT_scale=w1s[:, b * 128:(b + 1) * 128],
-                        rhs=hc[:].bitcast(FP8X4),
-                        rhs_scale=hs[:],
-                        start=True,
-                        stop=True,
-                    )
-                    nc.scalar.activation(
-                        out=hid_p[:, s, :], in_=hp[:], func=ACT.Relu, bias=b1f[:, b:b + 1], scale=1.0
-                    )
-                hid_g = work.tile([P, 4 * GT], BF16, align_bytes=64, tag="hid_g", bufs=3)
-                if gg == 1 or g % 2 == 1:
-                    nc.scalar.copy(
-                        out=hid_g[:].rearrange("p (c i t) -> p c t i", i=4, t=4),
-                        in_=hid_p[:].rearrange("p t (c i) -> p c t i", i=4),
-                    )
-                else:
-                    nc.vector.tensor_copy(
-                        out=hid_g[:].rearrange("p (c i t) -> p c t i", i=4, t=4),
-                        in_=hid_p[:].rearrange("p t (c i) -> p c t i", i=4),
-                    )
-                res.append(hid_g)
-            codes = []
-            for gg in range(2):
-                hid_c = work.tile([P, GT], U32, align_bytes=64, tag="hid_c", bufs=4)
-                hid_s = work.tile([P, GT], U8, align_bytes=64, tag="hid_s", bufs=4)
-                nc.vector.quantize_mx(out=hid_c[:].bitcast(FP8X4), scales=hid_s[:], in_=res[gg][:])
-                codes.append((hid_c, hid_s))
-            state[("b", g)] = codes
-
-        def stage_c(g):
-            hc, hs, hb = state[("a", g)]
-            codes = state[("b", g)]
-            s1 = work.tile([P, 4], F32, tag="s1", bufs=3)
-            s2 = work.tile([P, 4], F32, tag="s2", bufs=3)
-            negmu = work.tile([P, 4], F32, tag="negmu", bufs=3)
-            std = work.tile([P, 4], F32, tag="std", bufs=3)
-            rstd = work.tile([P, 4], F32, tag="rstd", bufs=3)
-            ot = work.tile([P, 4 * D], F32, tag="ot", bufs=2)
-            rs = []
-            for j in range(4):
-                fo = ps_c.tile([P, D], F32, tag="fo")
-                for gg in range(2):
-                    hid_c, hid_s = codes[gg]
-                    nc.tensor.matmul_mx(
-                        out=fo[:],
-                        lhsT=hid_c[:, j * 128:(j + 1) * 128].bitcast(FP8X4),
-                        lhsT_scale=hid_s[:, j * 128:(j + 1) * 128],
-                        rhs=w2c[:, gg * D:(gg + 1) * D].bitcast(FP8X4),
-                        rhs_scale=w2s[:, gg * D:(gg + 1) * D],
-                        start=(gg == 0),
-                        stop=(gg == 1),
-                    )
-                r = work.tile([P, D], F32, tag="r", bufs=8)
-                nc.vector.scalar_tensor_tensor(
-                    out=r[:], in0=fo[:], scalar=0.0, in1=hb[:, j, :], op0=ALU.add, op1=ALU.add,
-                    accum_out=s1[:, j:j + 1],
-                )
-                rs.append(r)
-            nc.vector.tensor_scalar(
-                out=negmu[:], in0=s1[:], scalar1=-1.0 / D, scalar2=None, op0=ALU.mult
-            )
-            for j in range(4):
-                junk = work.tile([P, D], BF16, tag="junk", bufs=2)
-                nc.scalar.activation(
-                    out=junk[:], in_=rs[j][:], func=ACT.Square, bias=negmu[:, j:j + 1], scale=1.0,
-                    accum_out=s2[:, j:j + 1],
-                )
-            nc.scalar.activation(out=std[:], in_=s2[:], func=ACT.Sqrt, bias=eps_t[:, 0:1], scale=1.0 / D)
-            nc.vector.reciprocal(out=rstd[:], in_=std[:])
-            for j in range(4):
-                t1 = work.tile([P, D], F32, tag="t1", bufs=4)
-                nc.vector.scalar_tensor_tensor(
-                    out=t1[:], in0=rs[j][:], scalar=negmu[:, j:j + 1], in1=cst[:, 0:D],
-                    op0=ALU.add, op1=ALU.mult,
-                )
-                nc.vector.scalar_tensor_tensor(
-                    out=ot[:, j * D:(j + 1) * D], in0=t1[:], scalar=rstd[:, j:j + 1], in1=cst[:, D:2 * D],
-                    op0=ALU.mult, op1=ALU.add,
-                )
-            nc.sync.dma_start(
-                out=o[g * GT:(g + 1) * GT, :].rearrange("(p j) d -> p (j d)", j=4), in_=ot[:]
+        def regroup_w2(half):
+            nc.vector.tensor_copy(
+                out=w2g[:, half * 2048:(half + 1) * 2048].rearrange("p (c i t) -> p c t i", i=4, t=4),
+                in_=w2raw[:, half].rearrange("p t (c i) -> p c t i", i=4),
             )
 
-        stage_a(0)
-        for gg in range(2):
+        def quantise_w2(half):
+            nc.vector.quantize_mx(
+                out=w2c[:, half * D:(half + 1) * D].bitcast(FP8X4),
+                scales=w2s[:, half * D:(half + 1) * D],
+                in_=w2g[:, half * 2048:(half + 1) * 2048],
+            )
+
+        live = {}
+
+        def absent(g):
+            return g < 0 or g >= GROUPS
+
+        def transpose_in(g, half):
+            if absent(g):
+                return
+            words = h_sb[g][:].bitcast(F32)
+            xt = next_bank("s")
+            live[("xt", g, half)] = xt
+            for jl in range(2):
+                j = 2 * half + jl
+                for u in range(2):
+                    nc.tensor.transpose(
+                        xt[:, u * 256 + jl * 128:u * 256 + jl * 128 + 128],
+                        words[:, j * 256 + u * 128:j * 256 + u * 128 + 128],
+                        ident[:],
+                    )
+
+        def copy_in(g, half):
+            if absent(g):
+                return
+            if half == 0:
+                live[("hg", g)] = work.tile([P, 4 * GROUP], BF16, align_bytes=64, tag="hg", name="hg", bufs=2)
+            pairs = live[("hg", g)][:].bitcast(F32).rearrange("q (c u) -> q c u", u=2)
             nc.scalar.copy(
-                out=w2g[:, gg * 2048:(gg + 1) * 2048].rearrange("p (c i t) -> p c t i", i=4, t=4),
-                in_=w2raw[:, gg].rearrange("p t (c i) -> p c t i", i=4),
+                out=pairs[:, half * 256:(half + 1) * 256, :],
+                in_=live[("xt", g, half)][:].rearrange("q (u c) -> q c u", u=2),
             )
-        for gg in range(2):
-            nc.vector.quantize_mx(
-                out=w2c[:, gg * D:(gg + 1) * D].bitcast(FP8X4),
-                scales=w2s[:, gg * D:(gg + 1) * D],
-                in_=w2g[:, gg * 2048:(gg + 1) * 2048],
+
+        def quantise_h(g):
+            if absent(g):
+                return
+            hc = work.tile([P, GROUP], U32, align_bytes=64, tag="hc", name="hc", bufs=3)
+            hs = work.tile([P, GROUP], U8, align_bytes=64, tag="hs", name="hs", bufs=3)
+            live[("hc", g)] = (hc, hs)
+            nc.vector.quantize_mx(out=hc[:].bitcast(FP8X4), scales=hs[:], in_=live[("hg", g)][:])
+
+        def first_matmul(g, b):
+            if absent(g):
+                return
+            hc, hs = live[("hc", g)]
+            hp = next_bank("s")
+            live[("hp", g, b)] = hp
+            nc.tensor.matmul_mx(
+                out=hp[:],
+                lhsT=w1c[:, b * 128:(b + 1) * 128].bitcast(FP8X4),
+                lhsT_scale=w1s[:, b * 128:(b + 1) * 128],
+                rhs=hc[:].bitcast(FP8X4),
+                rhs_scale=hs[:],
+                start=True,
+                stop=True,
             )
-        for step in range(1, NG + 2):
-            if step < NG:
-                stage_a(step)
-            if 1 <= step <= NG:
-                stage_b(step - 1)
-            if step >= 2:
-                stage_c(step - 2)
+
+        def relu_out(g, b):
+            if absent(g):
+                return
+            if b % 4 == 0:
+                live[("planes", g, b // 4)] = work.tile([P, 4, GROUP], BF16, tag="planes", name="planes", bufs=3)
+            nc.scalar.activation(
+                out=live[("planes", g, b // 4)][:, b % 4, :], in_=live[("hp", g, b)][:],
+                func=ACT.Relu, bias=b1f[:, b:b + 1], scale=1.0,
+            )
+
+        def regroup_hidden(g, half):
+            if absent(g):
+                return
+            hid_g = work.tile([P, 4 * GROUP], BF16, align_bytes=64, tag="hid_g", name="hid_g", bufs=3)
+            live[("hid_g", g, half)] = hid_g
+            copy = nc.vector.tensor_copy if half == 0 else nc.scalar.copy
+            copy(
+                out=hid_g[:].rearrange("p (c i t) -> p c t i", i=4, t=4),
+                in_=live[("planes", g, half)][:].rearrange("p t (c i) -> p c t i", i=4),
+            )
+
+        def quantise_hidden(g, half):
+            if absent(g):
+                return
+            hid_c = work.tile([P, GROUP], U32, align_bytes=64, tag="hid_c", name="hid_c", bufs=4)
+            hid_s = work.tile([P, GROUP], U8, align_bytes=64, tag="hid_s", name="hid_s", bufs=4)
+            live[("hid_c", g, half)] = (hid_c, hid_s)
+            nc.vector.quantize_mx(out=hid_c[:].bitcast(FP8X4), scales=hid_s[:], in_=live[("hid_g", g, half)][:])
+
+        def second_matmul(g, b):
+            if absent(g):
+                return
+            ft = next_bank("s")
+            live[("ft", g, b)] = ft
+            for half in range(2):
+                hid_c, hid_s = live[("hid_c", g, half)]
+                nc.tensor.matmul_mx(
+                    out=ft[:],
+                    lhsT=w2c[:, half * D + b * 128:half * D + (b + 1) * 128].bitcast(FP8X4),
+                    lhsT_scale=w2s[:, half * D + b * 128:half * D + (b + 1) * 128],
+                    rhs=hid_c[:].bitcast(FP8X4),
+                    rhs_scale=hid_s[:],
+                    start=(half == 0),
+                    stop=(half == 1),
+                )
+
+        def bias_out(g, b):
+            if absent(g):
+                return
+            if b == 0:
+                live[("x_t", g)] = work.tile([P, 4, GROUP], F32, tag="x_t", name="x_t", bufs=2)
+            nc.scalar.activation(
+                out=live[("x_t", g)][:, b, :], in_=live[("ft", g, b)][:],
+                func=ACT.Identity, bias=b2f[:, b:b + 1], scale=1.0,
+            )
+
+        def transpose_back(g, j):
+            if absent(g):
+                return
+            xb = next_bank("v")
+            live[("xb", g, j)] = xb
+            nc.tensor.matmul(out=xb[:], lhsT=identb[:], rhs=h_sb[g][:, j * D:(j + 1) * D], start=True, stop=False)
+            for b in range(4):
+                nc.tensor.matmul(
+                    out=xb[:, b * 128:(b + 1) * 128],
+                    lhsT=live[("x_t", g)][:, b, j * 128:(j + 1) * 128],
+                    rhs=ident[:],
+                    is_transpose=True,
+                    start=False,
+                    stop=(b == 3),
+                )
+
+        def mean_var(g, j):
+            if absent(g):
+                return
+            if j == 0:
+                live[("st", g)] = work.tile([P, TILES, 6], F32, tag="st", name="st", bufs=3)
+                live[("mv", g)] = work.tile([P, TILES, 2], F32, tag="mv", name="mv", bufs=3)
+            nc.vector.bn_stats(out=live[("st", g)][:, j, :], in_=live[("xb", g, j)][:])
+            nc.vector.bn_aggr(out=live[("mv", g)][:, j, :], in_=live[("st", g)][:, j, :])
+
+        def centre_gain(g, j):
+            if absent(g):
+                return
+            t1 = work.tile([P, D], F32, tag="t1", name="t1", bufs=8)
+            live[("t1", g, j)] = t1
+            nc.vector.scalar_tensor_tensor(
+                out=t1[:], in0=live[("xb", g, j)][:], scalar=live[("mv", g)][:, j, 0:1], in1=g2_bc[:],
+                op0=ALU.subtract, op1=ALU.mult,
+            )
+
+        def std_dev(g):
+            if absent(g):
+                return
+            std = work.tile([P, TILES], F32, tag="std", name="std", bufs=3)
+            live[("std", g)] = std
+            nc.scalar.activation(
+                out=std[:], in_=live[("mv", g)][:, :, 1], func=ACT.Sqrt, bias=eps_t[:, 0:1], scale=1.0
+            )
+
+        def one_over_std(g):
+            if absent(g):
+                return
+            rstd = work.tile([P, TILES], F32, tag="rstd", name="rstd", bufs=3)
+            live[("rstd", g)] = rstd
+            nc.vector.reciprocal(out=rstd[:], in_=live[("std", g)][:])
+
+        def scale_shift_store(g, j):
+            if absent(g):
+                return
+            if j % 2 == 0:
+                live[("ot", g)] = work.tile([P, 2 * D], F32, tag="ot", name="ot", bufs=4)
+            ot = live[("ot", g)]
+            nc.vector.scalar_tensor_tensor(
+                out=ot[:, (j % 2) * D:(j % 2 + 1) * D], in0=live[("t1", g, j)][:],
+                scalar=live[("rstd", g)][:, j:j + 1], in1=beta2_bc[:], op0=ALU.mult, op1=ALU.add,
+            )
+            if j % 2 == 1:
+                nc.sync.dma_start(
+                    out=o[g * GROUP:(g + 1) * GROUP, :].rearrange("(p j) d -> p j d", j=TILES)[:, j - 1:j + 1, :],
+                    in_=ot[:].rearrange("p (j d) -> p j d", j=2),
+                )
+
+        for i in range(-1, GROUPS + 2):
+            if i == -1:
+                regroup_w1(0, nc.vector.tensor_copy)
+                quantise_w1(0)
+            regroup_hidden(i - 1, 0)
+            quantise_hidden(i - 1, 0)
+            quantise_hidden(i - 1, 1)
+            transpose_in(i + 1, 0)
+            transpose_in(i + 1, 1)
+            relu_out(i, 0)
+            copy_in(i + 1, 0)
+            copy_in(i + 1, 1)
+            if i == -1:
+                regroup_w1(1, nc.scalar.copy)
+            for b in range(4):
+                second_matmul(i - 1, b)
+            bias_out(i - 1, 0)
+            bias_out(i - 1, 1)
+            mean_var(i - 2, 2)
+            mean_var(i - 2, 3)
+            std_dev(i - 2)
+            bias_out(i - 1, 2)
+            bias_out(i - 1, 3)
+            centre_gain(i - 2, 2)
+            centre_gain(i - 2, 3)
+            quantise_h(i + 1)
+            if i == -1:
+                quantise_w1(1)
+                regroup_w2(0)
+                regroup_w2(1)
+                quantise_w2(0)
+                quantise_w2(1)
+            one_over_std(i - 2)
+            for j in range(TILES):
+                scale_shift_store(i - 2, j)
+            for b in range(1, 5):
+                first_matmul(i, b)
+            for b in range(1, 5):
+                relu_out(i, b)
+            transpose_back(i - 1, 0)
+            for b in range(5, 8):
+                first_matmul(i, b)
+            for b in range(5, 8):
+                relu_out(i, b)
+            transpose_back(i - 1, 1)
+            mean_var(i - 1, 0)
+            centre_gain(i - 1, 0)
+            first_matmul(i + 1, 0)
+            transpose_back(i - 1, 2)
+            mean_var(i - 1, 1)
+            centre_gain(i - 1, 1)
+            transpose_back(i - 1, 3)
+            regroup_hidden(i, 1)

@@ -42,16 +42,14 @@ def tile_ffnn_encoder_pc_t_kernel(tc, h_attn, W1, b1, W2, b2, g2, beta2, out):
             ring_next[ring] += 1
             return psum.tile([P, cols], dtype, tag="%s%d" % (ring, k), name="%s%d" % (ring, k))
 
-        eps_t = keep.tile([P, 1], F32)
-        nc.vector.memset(eps_t[:], EPS)
-        warm = keep.tile([P, 1], F32)
-        nc.scalar.activation(out=warm[:], in_=eps_t[:], func=ACT.Sqrt)
-        ones = keep.tile([P, P], BF16)
-        nc.vector.memset(ones[:], 1.0)
         rows = keep.tile([P, 2 * D], BF16)
         nc.vector.memset(rows[:], 0.0)
         b2rows = keep.tile([P, P], BF16)
         nc.vector.memset(b2rows[:], 0.0)
+        eps_t = keep.tile([P, 1], F32)
+        nc.vector.memset(eps_t[:], EPS)
+        ones = keep.tile([P, P], BF16)
+        nc.vector.memset(ones[:], 1.0)
         ident = keep.tile([P, P], F32)
         make_identity(nc, ident[:])
         identb = keep.tile([P, P], BF16)
@@ -59,9 +57,11 @@ def tile_ffnn_encoder_pc_t_kernel(tc, h_attn, W1, b1, W2, b2, g2, beta2, out):
 
         b1raw = keep.tile([P, 2, 4], BF16)
         nc.scalar.dma_start(out=b1raw[:], in_=b1.rearrange("(g p t) -> p g t", g=2, t=4))
+        nc.scalar.dma_start(out=b2rows[0:4, :], in_=b2.rearrange("(b p) -> b p", b=4))
         nc.scalar.dma_start(out=rows[0:1, 0:D], in_=g2.rearrange("(o d) -> o d", o=1))
         nc.scalar.dma_start(out=rows[0:1, D:2 * D], in_=beta2.rearrange("(o d) -> o d", o=1))
-        nc.scalar.dma_start(out=b2rows[0:4, :], in_=b2.rearrange("(b p) -> b p", b=4))
+        warm = keep.tile([P, 1], F32)
+        nc.scalar.activation(out=warm[:], in_=eps_t[:], func=ACT.Sqrt)
 
         h_sb = [keep.tile([P, TILES * D], BF16, name="h%d" % g) for g in range(GROUPS)]
         w1raw = keep.tile([P, 4, F], BF16)
@@ -95,18 +95,18 @@ def tile_ffnn_encoder_pc_t_kernel(tc, h_attn, W1, b1, W2, b2, g2, beta2, out):
             load_h(g)
 
         b1f = keep.tile([P, 8], F32)
-        nc.vector.tensor_copy(out=b1f[:], in_=b1raw[:].rearrange("p g t -> p (g t)"))
-
         beta2_bc = psum.tile([P, D], BF16, tag="beta2", name="beta2_bc")
-        nc.tensor.matmul(out=beta2_bc[:], lhsT=ones[:], rhs=rows[:, D:2 * D], start=True, stop=True)
-        g2_ps = next_bank("s")
-        nc.tensor.matmul(out=g2_ps[:], lhsT=ones[:], rhs=rows[:, 0:D], start=True, stop=True)
         g2_bc = keep.tile([P, D], F32)
-        nc.vector.tensor_copy(out=g2_bc[:], in_=g2_ps[:])
-        b2_ps = next_bank("s", BF16, P)
-        nc.tensor.transpose(b2_ps[:], b2rows[:], identb[:])
         b2f = keep.tile([P, 4], F32)
-        nc.vector.tensor_copy(out=b2f[:], in_=b2_ps[:, 0:4])
+
+        def spread_vectors():
+            nc.tensor.matmul(out=beta2_bc[:], lhsT=ones[:], rhs=rows[:, D:2 * D], start=True, stop=True)
+            g2_ps = next_bank("v")
+            nc.tensor.matmul(out=g2_ps[:], lhsT=ones[:], rhs=rows[:, 0:D], start=True, stop=True)
+            nc.vector.tensor_copy(out=g2_bc[:], in_=g2_ps[:])
+            b2_ps = next_bank("v", BF16, P)
+            nc.tensor.transpose(b2_ps[:], b2rows[:], identb[:])
+            nc.vector.tensor_copy(out=b2f[:], in_=b2_ps[:, 0:4])
 
         w1g = keep.tile([P, 4 * F], BF16, align_bytes=64)
         w1c = keep.tile([P, F], U32, align_bytes=64)
@@ -323,50 +323,52 @@ def tile_ffnn_encoder_pc_t_kernel(tc, h_attn, W1, b1, W2, b2, g2, beta2, out):
             if i == -1:
                 regroup_w1(0, nc.vector.tensor_copy)
                 quantise_w1(0)
-            regroup_hidden(i - 1, 0)
-            quantise_hidden(i - 1, 0)
+                nc.vector.tensor_copy(out=b1f[:], in_=b1raw[:].rearrange("p g t -> p (g t)"))
             quantise_hidden(i - 1, 1)
+            for b in range(4):
+                second_matmul(i - 1, b)
+            for b in range(5):
+                relu_out(i, b)
+            mean_var(i - 2, 2)
+            mean_var(i - 2, 3)
+            centre_gain(i - 2, 2)
+            regroup_hidden(i, 0)
+            bias_out(i - 1, 0)
+            bias_out(i - 1, 1)
+            std_dev(i - 2)
+            bias_out(i - 1, 2)
+            bias_out(i - 1, 3)
+            centre_gain(i - 2, 3)
+            quantise_hidden(i, 0)
+            one_over_std(i - 2)
+            for j in range(3):
+                scale_shift_store(i - 2, j)
             transpose_in(i + 1, 0)
             transpose_in(i + 1, 1)
-            relu_out(i, 0)
             copy_in(i + 1, 0)
             copy_in(i + 1, 1)
             if i == -1:
                 regroup_w1(1, nc.scalar.copy)
-            for b in range(4):
-                second_matmul(i - 1, b)
-            bias_out(i - 1, 0)
-            bias_out(i - 1, 1)
-            mean_var(i - 2, 2)
-            mean_var(i - 2, 3)
-            std_dev(i - 2)
-            bias_out(i - 1, 2)
-            bias_out(i - 1, 3)
-            centre_gain(i - 2, 2)
-            centre_gain(i - 2, 3)
             quantise_h(i + 1)
+            scale_shift_store(i - 2, 3)
             if i == -1:
                 quantise_w1(1)
                 regroup_w2(0)
                 regroup_w2(1)
                 quantise_w2(0)
                 quantise_w2(1)
-            one_over_std(i - 2)
-            for j in range(TILES):
-                scale_shift_store(i - 2, j)
-            for b in range(1, 5):
+            for b in range(5, 8):
                 first_matmul(i, b)
-            for b in range(1, 5):
+            for b in range(5, 8):
                 relu_out(i, b)
             transpose_back(i - 1, 0)
-            for b in range(5, 8):
-                first_matmul(i, b)
-            for b in range(5, 8):
-                relu_out(i, b)
             transpose_back(i - 1, 1)
             mean_var(i - 1, 0)
             centre_gain(i - 1, 0)
-            first_matmul(i + 1, 0)
+            for b in range(5):
+                first_matmul(i + 1, b)
+            if i == -1:
+                spread_vectors()
             transpose_back(i - 1, 2)
             mean_var(i - 1, 1)
             centre_gain(i - 1, 1)

@@ -211,10 +211,10 @@ def tile_ffnn_encoder_pc_t_kernel(tc, h_attn, W1, b1, W2, b2, g2, beta2, out):
                 return
             hid_g = work.tile([P, 4 * GROUP], BF16, align_bytes=64, tag="hid_g", name="hid_g", bufs=3)
             live[("hid_g", g, half)] = hid_g
-            copy = nc.vector.tensor_copy if half == 0 else nc.scalar.copy
-            copy(
-                out=hid_g[:].rearrange("p (c i t) -> p c t i", i=4, t=4),
-                in_=live[("planes", g, half)][:].rearrange("p t (c i) -> p c t i", i=4),
+            nc.gpsimd.tensor_scalar(
+                out=hid_g[:].rearrange("p (c t) -> p c t", t=4),
+                in0=live[("planes", g, half)][:].rearrange("p t c -> p c t"),
+                scalar1=1.0, scalar2=0.0, op0=ALU.mult, op1=ALU.add,
             )
 
         def quantise_hidden(g, half):
@@ -324,24 +324,35 @@ def tile_ffnn_encoder_pc_t_kernel(tc, h_attn, W1, b1, W2, b2, g2, beta2, out):
                 regroup_w1(0, nc.vector.tensor_copy)
                 quantise_w1(0)
                 nc.vector.tensor_copy(out=b1f[:], in_=b1raw[:].rearrange("p g t -> p (g t)"))
-            quantise_hidden(i - 1, 1)
+            first_matmul(i, 5)
+            first_matmul(i, 6)
             for b in range(4):
-                second_matmul(i - 1, b)
-            for b in range(5):
                 relu_out(i, b)
-            mean_var(i - 2, 2)
-            mean_var(i - 2, 3)
-            centre_gain(i - 2, 2)
             regroup_hidden(i, 0)
+            mean_var(i - 2, 0)
+            centre_gain(i - 2, 0)
+            transpose_back(i - 2, 2)
+            first_matmul(i, 7)
+            second_matmul(i - 1, 0)
+            mean_var(i - 2, 1)
+            centre_gain(i - 2, 1)
+            transpose_back(i - 2, 3)
+            for b in range(1, 4):
+                second_matmul(i - 1, b)
+            for b in range(4, 8):
+                relu_out(i, b)
+            regroup_hidden(i, 1)
+            mean_var(i - 2, 2)
+            centre_gain(i - 2, 2)
+            mean_var(i - 2, 3)
+            centre_gain(i - 2, 3)
             bias_out(i - 1, 0)
             bias_out(i - 1, 1)
             std_dev(i - 2)
             bias_out(i - 1, 2)
             bias_out(i - 1, 3)
-            centre_gain(i - 2, 3)
-            quantise_hidden(i, 0)
             one_over_std(i - 2)
-            for j in range(3):
+            for j in range(TILES):
                 scale_shift_store(i - 2, j)
             transpose_in(i + 1, 0)
             transpose_in(i + 1, 1)
@@ -350,27 +361,17 @@ def tile_ffnn_encoder_pc_t_kernel(tc, h_attn, W1, b1, W2, b2, g2, beta2, out):
             if i == -1:
                 regroup_w1(1, nc.scalar.copy)
             quantise_h(i + 1)
-            scale_shift_store(i - 2, 3)
+            quantise_hidden(i, 0)
+            quantise_hidden(i, 1)
             if i == -1:
                 quantise_w1(1)
                 regroup_w2(0)
                 regroup_w2(1)
                 quantise_w2(0)
                 quantise_w2(1)
-            for b in range(5, 8):
-                first_matmul(i, b)
-            for b in range(5, 8):
-                relu_out(i, b)
             transpose_back(i - 1, 0)
             transpose_back(i - 1, 1)
-            mean_var(i - 1, 0)
-            centre_gain(i - 1, 0)
             for b in range(5):
                 first_matmul(i + 1, b)
             if i == -1:
                 spread_vectors()
-            transpose_back(i - 1, 2)
-            mean_var(i - 1, 1)
-            centre_gain(i - 1, 1)
-            transpose_back(i - 1, 3)
-            regroup_hidden(i, 1)

@@ -209,7 +209,7 @@ def tile_ffnn_encoder_pc_t_kernel(tc, h_attn, W1, b1, W2, b2, g2, beta2, out):
         def regroup_hidden(g, half):
             if absent(g):
                 return
-            hid_g = work.tile([P, 4 * GROUP], BF16, align_bytes=64, tag="hid_g", name="hid_g", bufs=3)
+            hid_g = work.tile([P, 4 * GROUP], BF16, align_bytes=64, tag="hid_g", name="hid_g", bufs=1)
             live[("hid_g", g, half)] = hid_g
             nc.gpsimd.tensor_scalar(
                 out=hid_g[:].rearrange("p (c t) -> p c t", t=4),
@@ -324,33 +324,21 @@ def tile_ffnn_encoder_pc_t_kernel(tc, h_attn, W1, b1, W2, b2, g2, beta2, out):
                 regroup_w1(0, nc.vector.tensor_copy)
                 quantise_w1(0)
                 nc.vector.tensor_copy(out=b1f[:], in_=b1raw[:].rearrange("p g t -> p (g t)"))
-            first_matmul(i, 5)
-            first_matmul(i, 6)
+            quantise_hidden(i - 1, 1)
+            for b in range(4):
+                second_matmul(i - 1, b)
             for b in range(4):
                 relu_out(i, b)
             regroup_hidden(i, 0)
-            mean_var(i - 2, 0)
-            centre_gain(i - 2, 0)
-            transpose_back(i - 2, 2)
-            first_matmul(i, 7)
-            second_matmul(i - 1, 0)
-            mean_var(i - 2, 1)
-            centre_gain(i - 2, 1)
-            transpose_back(i - 2, 3)
-            for b in range(1, 4):
-                second_matmul(i - 1, b)
-            for b in range(4, 8):
-                relu_out(i, b)
-            regroup_hidden(i, 1)
+            relu_out(i, 4)
             mean_var(i - 2, 2)
-            centre_gain(i - 2, 2)
             mean_var(i - 2, 3)
+            centre_gain(i - 2, 2)
             centre_gain(i - 2, 3)
             bias_out(i - 1, 0)
-            bias_out(i - 1, 1)
             std_dev(i - 2)
-            bias_out(i - 1, 2)
-            bias_out(i - 1, 3)
+            for b in range(1, 4):
+                bias_out(i - 1, b)
             one_over_std(i - 2)
             for j in range(TILES):
                 scale_shift_store(i - 2, j)
@@ -360,18 +348,28 @@ def tile_ffnn_encoder_pc_t_kernel(tc, h_attn, W1, b1, W2, b2, g2, beta2, out):
             copy_in(i + 1, 1)
             if i == -1:
                 regroup_w1(1, nc.scalar.copy)
-            quantise_h(i + 1)
             quantise_hidden(i, 0)
-            quantise_hidden(i, 1)
+            quantise_h(i + 1)
             if i == -1:
                 quantise_w1(1)
                 regroup_w2(0)
                 regroup_w2(1)
                 quantise_w2(0)
                 quantise_w2(1)
+            for b in range(5, 8):
+                first_matmul(i, b)
+            for b in range(5, 8):
+                relu_out(i, b)
+            regroup_hidden(i, 1)
             transpose_back(i - 1, 0)
             transpose_back(i - 1, 1)
+            mean_var(i - 1, 0)
+            centre_gain(i - 1, 0)
             for b in range(5):
                 first_matmul(i + 1, b)
             if i == -1:
                 spread_vectors()
+            transpose_back(i - 1, 2)
+            mean_var(i - 1, 1)
+            centre_gain(i - 1, 1)
+            transpose_back(i - 1, 3)

@@ -61,7 +61,7 @@ def tile_ffnn_encoder_pc_t_kernel(tc, h_attn, W1, b1, W2, b2, g2, beta2, out):
         nc.scalar.dma_start(out=rows[0:1, 0:D], in_=g2.rearrange("(o d) -> o d", o=1))
         nc.scalar.dma_start(out=rows[0:1, D:2 * D], in_=beta2.rearrange("(o d) -> o d", o=1))
         warm = keep.tile([P, 1], F32)
-        nc.scalar.activation(out=warm[:], in_=eps_t[:], func=ACT.Sqrt)
+        nc.scalar.activation(out=warm[:], in_=eps_t[:], func=ACT.Abs_reciprocal_sqrt)
 
         h_sb = [keep.tile([P, TILES * D], BF16, name="h%d" % g) for g in range(GROUPS)]
         w1raw = keep.tile([P, 4, F], BF16)
@@ -211,11 +211,18 @@ def tile_ffnn_encoder_pc_t_kernel(tc, h_attn, W1, b1, W2, b2, g2, beta2, out):
                 return
             hid_g = work.tile([P, 4 * GROUP], BF16, align_bytes=64, tag="hid_g", name="hid_g", bufs=1)
             live[("hid_g", g, half)] = hid_g
+            planes = live[("planes", g, half)]
+            cut = GROUP if half == 0 else GROUP // 2
             nc.gpsimd.tensor_scalar(
-                out=hid_g[:].rearrange("p (c t) -> p c t", t=4),
-                in0=live[("planes", g, half)][:].rearrange("p t c -> p c t"),
+                out=hid_g[:, 0:4 * cut].rearrange("p (c t) -> p c t", t=4),
+                in0=planes[:, :, 0:cut].rearrange("p t c -> p c t"),
                 scalar1=1.0, scalar2=0.0, op0=ALU.mult, op1=ALU.add,
             )
+            if cut < GROUP:
+                nc.scalar.copy(
+                    out=hid_g[:, 4 * cut:].rearrange("p (c i t) -> p c t i", i=4, t=4),
+                    in_=planes[:, :, cut:].rearrange("p t (c i) -> p c t i", i=4),
+                )
 
         def quantise_hidden(g, half):
             if absent(g):
@@ -287,21 +294,15 @@ def tile_ffnn_encoder_pc_t_kernel(tc, h_attn, W1, b1, W2, b2, g2, beta2, out):
                 op0=ALU.subtract, op1=ALU.mult,
             )
 
-        def std_dev(g):
-            if absent(g):
-                return
-            std = work.tile([P, TILES], F32, tag="std", name="std", bufs=3)
-            live[("std", g)] = std
-            nc.scalar.activation(
-                out=std[:], in_=live[("mv", g)][:, :, 1], func=ACT.Sqrt, bias=eps_t[:, 0:1], scale=1.0
-            )
-
         def one_over_std(g):
             if absent(g):
                 return
             rstd = work.tile([P, TILES], F32, tag="rstd", name="rstd", bufs=3)
             live[("rstd", g)] = rstd
-            nc.vector.reciprocal(out=rstd[:], in_=live[("std", g)][:])
+            nc.scalar.activation(
+                out=rstd[:], in_=live[("mv", g)][:, :, 1], func=ACT.Abs_reciprocal_sqrt,
+                bias=eps_t[:, 0:1], scale=1.0,
+            )
 
         def scale_shift_store(g, j):
             if absent(g):
@@ -336,21 +337,19 @@ def tile_ffnn_encoder_pc_t_kernel(tc, h_attn, W1, b1, W2, b2, g2, beta2, out):
             centre_gain(i - 2, 2)
             centre_gain(i - 2, 3)
             bias_out(i - 1, 0)
-            std_dev(i - 2)
+            one_over_std(i - 2)
             for b in range(1, 4):
                 bias_out(i - 1, b)
-            one_over_std(i - 2)
             for j in range(TILES):
                 scale_shift_store(i - 2, j)
             transpose_in(i + 1, 0)
             transpose_in(i + 1, 1)
             copy_in(i + 1, 0)
             copy_in(i + 1, 1)
-            if i == -1:
-                regroup_w1(1, nc.scalar.copy)
             quantise_hidden(i, 0)
             quantise_h(i + 1)
             if i == -1:
+                regroup_w1(1, nc.vector.tensor_copy)
                 quantise_w1(1)
                 regroup_w2(0)
                 regroup_w2(1)

@@ -32,7 +32,6 @@ def tile_ffnn_encoder_pc_t_kernel(tc, h_attn, W1, b1, W2, b2, g2, beta2, out):
         keep = ctx.enter_context(tc.tile_pool(name="keep", bufs=1))
         work = ctx.enter_context(tc.tile_pool(name="work", bufs=2))
         psum = ctx.enter_context(tc.psum_pool(name="psum", bufs=1))
-        ctx.enter_context(tc.manual_schedule())
 
         ring_size = {"s": 5, "v": 2}
         ring_next = {"s": 0, "v": 0}

@@ -22,6 +22,8 @@ GROUP = 512
 TILES = GROUP // P
 GROUPS = TOKENS // GROUP
 BANK = 512
+CHUNK = 256
+OFF = (1,)
 
 
 def tile_ffnn_encoder_pc_t_kernel(tc, h_attn, W1, b1, W2, b2, g2, beta2, out):
@@ -32,8 +34,9 @@ def tile_ffnn_encoder_pc_t_kernel(tc, h_attn, W1, b1, W2, b2, g2, beta2, out):
         keep = ctx.enter_context(tc.tile_pool(name="keep", bufs=1))
         work = ctx.enter_context(tc.tile_pool(name="work", bufs=2))
         psum = ctx.enter_context(tc.psum_pool(name="psum", bufs=1))
+        ctx.enter_context(tc.manual_schedule())
 
-        ring_size = {"s": 5, "v": 2}
+        ring_size = {"s": 4, "v": 3}
         ring_next = {"s": 0, "v": 0}
 
         def next_bank(ring, dtype=F32, cols=BANK):
@@ -84,18 +87,18 @@ def tile_ffnn_encoder_pc_t_kernel(tc, h_attn, W1, b1, W2, b2, g2, beta2, out):
         load_h(0)
         load_w1(0)
         load_w1(1)
-        load_h(1)
         for half in range(2):
             nc.sync.dma_start(
                 out=w2raw[:, half],
                 in_=W2[512 * half:512 * half + 512, :].rearrange("(p t) d -> p t d", t=4),
             )
-        for g in range(2, GROUPS):
+        for g in range(1, GROUPS):
             load_h(g)
 
         b1f = keep.tile([P, 8], F32)
         beta2_bc = psum.tile([P, D], BF16, tag="beta2", name="beta2_bc")
         g2_bc = keep.tile([P, D], F32)
+        beta2_sb = keep.tile([P, D], F32)
         b2f = keep.tile([P, 4], F32)
 
         def spread_vectors():
@@ -103,9 +106,18 @@ def tile_ffnn_encoder_pc_t_kernel(tc, h_attn, W1, b1, W2, b2, g2, beta2, out):
             g2_ps = next_bank("v")
             nc.tensor.matmul(out=g2_ps[:], lhsT=ones[:], rhs=rows[:, 0:D], start=True, stop=True)
             nc.vector.tensor_copy(out=g2_bc[:], in_=g2_ps[:])
+            nc.scalar.copy(out=beta2_sb[:], in_=beta2_bc[:])
             b2_ps = next_bank("v", BF16, P)
             nc.tensor.transpose(b2_ps[:], b2rows[:], identb[:])
             nc.vector.tensor_copy(out=b2f[:], in_=b2_ps[:, 0:4])
+
+        def regroup(engine, out, in_):
+            if engine == "gpsimd":
+                nc.gpsimd.tensor_scalar(out=out, in0=in_, scalar1=1.0, scalar2=0.0, op0=ALU.mult, op1=ALU.add)
+            elif engine == "vector":
+                nc.vector.tensor_copy(out=out, in_=in_)
+            else:
+                nc.scalar.copy(out=out, in_=in_)
 
         w1g = keep.tile([P, 4 * F], BF16, align_bytes=64)
         w1c = keep.tile([P, F], U32, align_bytes=64)
@@ -114,10 +126,12 @@ def tile_ffnn_encoder_pc_t_kernel(tc, h_attn, W1, b1, W2, b2, g2, beta2, out):
         w2c = keep.tile([P, 2 * D], U32, align_bytes=64)
         w2s = keep.tile([P, 2 * D], U8, align_bytes=64)
 
-        def regroup_w1(half, copy):
-            copy(
-                out=w1g[:, half * 2048:(half + 1) * 2048].rearrange("q (s p t) -> q s p t", s=4, t=4),
-                in_=w1raw[:, :, half * 512:(half + 1) * 512].rearrange("q t (p s) -> q s p t", s=4),
+        def regroup_w1(half, s, engine):
+            block = 4 * half + s
+            regroup(
+                engine,
+                w1g[:, block * 512:(block + 1) * 512].rearrange("q (p t) -> q p t", t=4),
+                w1raw[:, :, half * 512:(half + 1) * 512].rearrange("q t (p s) -> q s p t", s=4)[:, s],
             )
 
         def quantise_w1(half):
@@ -127,10 +141,12 @@ def tile_ffnn_encoder_pc_t_kernel(tc, h_attn, W1, b1, W2, b2, g2, beta2, out):
                 in_=w1g[:, half * 2048:(half + 1) * 2048],
             )
 
-        def regroup_w2(half):
-            nc.vector.tensor_copy(
-                out=w2g[:, half * 2048:(half + 1) * 2048].rearrange("p (c i t) -> p c t i", i=4, t=4),
-                in_=w2raw[:, half].rearrange("p t (c i) -> p c t i", i=4),
+        def regroup_w2(half, quarter, engine):
+            lo = quarter * 256
+            regroup(
+                engine,
+                w2g[:, half * 2048 + 4 * lo:half * 2048 + 4 * lo + 1024].rearrange("p (c i t) -> p c t i", i=4, t=4),
+                w2raw[:, half, :, lo:lo + 256].rearrange("p t (c i) -> p c t i", i=4),
             )
 
         def quantise_w2(half):
@@ -179,11 +195,11 @@ def tile_ffnn_encoder_pc_t_kernel(tc, h_attn, W1, b1, W2, b2, g2, beta2, out):
             live[("hc", g)] = (hc, hs)
             nc.vector.quantize_mx(out=hc[:].bitcast(FP8X4), scales=hs[:], in_=live[("hg", g)][:])
 
-        def first_matmul(g, b):
+        def first_matmul(g, b, ring="s"):
             if absent(g):
                 return
             hc, hs = live[("hc", g)]
-            hp = next_bank("s")
+            hp = next_bank(ring)
             live[("hp", g, b)] = hp
             nc.tensor.matmul_mx(
                 out=hp[:],
@@ -195,32 +211,39 @@ def tile_ffnn_encoder_pc_t_kernel(tc, h_attn, W1, b1, W2, b2, g2, beta2, out):
                 stop=True,
             )
 
-        def relu_out(g, b):
+        def relu_out(g, b, engine="scalar"):
             if absent(g):
                 return
             if b % 4 == 0:
                 live[("planes", g, b // 4)] = work.tile([P, 4, GROUP], BF16, tag="planes", name="planes", bufs=3)
-            nc.scalar.activation(
-                out=live[("planes", g, b // 4)][:, b % 4, :], in_=live[("hp", g, b)][:],
-                func=ACT.Relu, bias=b1f[:, b:b + 1], scale=1.0,
-            )
+            out = live[("planes", g, b // 4)][:, b % 4, :]
+            if engine == "scalar":
+                nc.scalar.activation(
+                    out=out, in_=live[("hp", g, b)][:], func=ACT.Relu, bias=b1f[:, b:b + 1], scale=1.0,
+                )
+            else:
+                nc.vector.tensor_scalar(
+                    out=out, in0=live[("hp", g, b)][:], scalar1=b1f[:, b:b + 1], scalar2=0.0,
+                    op0=ALU.add, op1=ALU.max,
+                )
 
-        def regroup_hidden(g, half):
+        def regroup_hidden(g, half, engine="gpsimd", lo=0, hi=GROUP):
             if absent(g):
                 return
-            hid_g = work.tile([P, 4 * GROUP], BF16, align_bytes=64, tag="hid_g", name="hid_g", bufs=1)
-            live[("hid_g", g, half)] = hid_g
-            planes = live[("planes", g, half)]
-            cut = GROUP if half == 0 else GROUP // 2
-            nc.gpsimd.tensor_scalar(
-                out=hid_g[:, 0:4 * cut].rearrange("p (c t) -> p c t", t=4),
-                in0=planes[:, :, 0:cut].rearrange("p t c -> p c t"),
-                scalar1=1.0, scalar2=0.0, op0=ALU.mult, op1=ALU.add,
-            )
-            if cut < GROUP:
-                nc.scalar.copy(
-                    out=hid_g[:, 4 * cut:].rearrange("p (c i t) -> p c t i", i=4, t=4),
-                    in_=planes[:, :, cut:].rearrange("p t (c i) -> p c t i", i=4),
+            if lo == 0:
+                live[("hid_g", g, half)] = work.tile([P, 4 * GROUP], BF16, align_bytes=64, tag="hid_g", name="hid_g", bufs=2)
+            if engine == "gpsimd":
+                for c in range(lo, hi, CHUNK):
+                    regroup(
+                        engine,
+                        live[("hid_g", g, half)][:, 4 * c:4 * (c + CHUNK)].rearrange("p (c t) -> p c t", t=4),
+                        live[("planes", g, half)][:, :, c:c + CHUNK].rearrange("p t c -> p c t"),
+                    )
+            else:
+                regroup(
+                    engine,
+                    live[("hid_g", g, half)][:, 4 * lo:4 * hi].rearrange("p (c i t) -> p c t i", i=4, t=4),
+                    live[("planes", g, half)][:, :, lo:hi].rearrange("p t (c i) -> p c t i", i=4),
                 )
 
         def quantise_hidden(g, half):
@@ -274,100 +297,150 @@ def tile_ffnn_encoder_pc_t_kernel(tc, h_attn, W1, b1, W2, b2, g2, beta2, out):
                     stop=(b == 3),
                 )
 
-        def mean_var(g, j):
+        def stats(n):
+            g, j = divmod(n, TILES)
             if absent(g):
                 return
             if j == 0:
-                live[("st", g)] = work.tile([P, TILES, 6], F32, tag="st", name="st", bufs=3)
                 live[("mv", g)] = work.tile([P, TILES, 2], F32, tag="mv", name="mv", bufs=3)
-            nc.vector.bn_stats(out=live[("st", g)][:, j, :], in_=live[("xb", g, j)][:])
-            nc.vector.bn_aggr(out=live[("mv", g)][:, j, :], in_=live[("st", g)][:, j, :])
+            st = work.tile([P, 6], F32, tag="st", name="st", bufs=6)
+            live[("st", n)] = st
+            nc.vector.bn_stats(out=st[:], in_=live[("xb", g, j)][:])
 
-        def centre_gain(g, j):
+        def aggregate(n):
+            g, j = divmod(n, TILES)
+            if absent(g):
+                return
+            nc.vector.bn_aggr(out=live[("mv", g)][:, j, :], in_=live[("st", n)][:])
+
+        def centre_gain(n):
+            g, j = divmod(n, TILES)
             if absent(g):
                 return
             t1 = work.tile([P, D], F32, tag="t1", name="t1", bufs=8)
-            live[("t1", g, j)] = t1
+            live[("t1", n)] = t1
             nc.vector.scalar_tensor_tensor(
                 out=t1[:], in0=live[("xb", g, j)][:], scalar=live[("mv", g)][:, j, 0:1], in1=g2_bc[:],
                 op0=ALU.subtract, op1=ALU.mult,
             )
 
-        def one_over_std(g):
+        def one_over_std(g, half):
             if absent(g):
                 return
-            rstd = work.tile([P, TILES], F32, tag="rstd", name="rstd", bufs=3)
-            live[("rstd", g)] = rstd
+            rstd = work.tile([P, 2], F32, tag="rstd", name="rstd", bufs=6)
+            live[("rstd", g, half)] = rstd
             nc.scalar.activation(
-                out=rstd[:], in_=live[("mv", g)][:, :, 1], func=ACT.Abs_reciprocal_sqrt,
+                out=rstd[:], in_=live[("mv", g)][:, 2 * half:2 * half + 2, 1], func=ACT.Abs_reciprocal_sqrt,
                 bias=eps_t[:, 0:1], scale=1.0,
             )
 
-        def scale_shift_store(g, j):
+        def scale(n):
+            g, j = divmod(n, TILES)
+            if absent(g):
+                return
+            t2 = work.tile([P, D], F32, tag="t2", name="t2", bufs=4)
+            live[("t2", n)] = t2
+            nc.scalar.activation(
+                out=t2[:], in_=live[("t1", n)][:], func=ACT.Copy, scale=live[("rstd", g, j // 2)][:, j % 2:j % 2 + 1],
+            )
+
+        def scale_shift_store(n):
+            g, j = divmod(n, TILES)
             if absent(g):
                 return
             if j % 2 == 0:
                 live[("ot", g)] = work.tile([P, 2 * D], F32, tag="ot", name="ot", bufs=4)
             ot = live[("ot", g)]
-            nc.vector.scalar_tensor_tensor(
-                out=ot[:, (j % 2) * D:(j % 2 + 1) * D], in0=live[("t1", g, j)][:],
-                scalar=live[("rstd", g)][:, j:j + 1], in1=beta2_bc[:], op0=ALU.mult, op1=ALU.add,
-            )
+            if ("t2", n) in live:
+                nc.gpsimd.tensor_tensor(out=ot[:, (j % 2) * D:(j % 2 + 1) * D], in0=live[("t2", n)][:], in1=beta2_sb[:], op=ALU.add)
+            else:
+                nc.vector.scalar_tensor_tensor(
+                    out=ot[:, (j % 2) * D:(j % 2 + 1) * D], in0=live[("t1", n)][:],
+                    scalar=live[("rstd", g, j // 2)][:, j % 2:j % 2 + 1], in1=beta2_bc[:], op0=ALU.mult, op1=ALU.add,
+                )
             if j % 2 == 1:
                 nc.sync.dma_start(
                     out=o[g * GROUP:(g + 1) * GROUP, :].rearrange("(p j) d -> p j d", j=TILES)[:, j - 1:j + 1, :],
                     in_=ot[:].rearrange("p (j d) -> p j d", j=2),
                 )
 
-        for i in range(-1, GROUPS + 2):
-            if i == -1:
-                regroup_w1(0, nc.vector.tensor_copy)
-                quantise_w1(0)
-                nc.vector.tensor_copy(out=b1f[:], in_=b1raw[:].rearrange("p g t -> p (g t)"))
-            quantise_hidden(i - 1, 1)
+        def slot(n, lag=4):
+            stats(n)
+            centre_gain(n - 1)
+            aggregate(n)
+            scale_shift_store(n - lag)
+
+        transpose_in(0, 0)
+        transpose_in(0, 1)
+        copy_in(0, 0)
+        copy_in(0, 1)
+        spread_vectors()
+        nc.vector.tensor_copy(out=b1f[:], in_=b1raw[:].rearrange("p g t -> p (g t)"))
+        quantise_h(0)
+        for half in range(2):
+            for s in range(3):
+                regroup_w1(half, s, "vector")
+            regroup_w1(half, 3, "scalar")
+            if half == 0:
+                quantise_w1(half)
+        regroup_w2(0, 0, "scalar")
+        for b in range(4):
+            first_matmul(0, b, "sv"[b % 2])
+        for b in range(4):
+            relu_out(0, b, ("scalar", "vector")[b % 2])
+        regroup_w2(1, 0, "gpsimd")
+        quantise_w1(1)
+        regroup_hidden(0, 0, "vector")
+        transpose_in(1, 0)
+        transpose_in(1, 1)
+        for b in range(4, 8):
+            first_matmul(0, b)
+            relu_out(0, b)
+            if b == 5:
+                copy_in(1, 0)
+                copy_in(1, 1)
+        regroup_w2(0, 1, "vector")
+        quantise_hidden(0, 0)
+        quantise_h(1)
+        regroup_w2(1, 1, "gpsimd")
+        regroup_hidden(0, 1, "vector")
+        quantise_w2(0)
+        quantise_w2(1)
+        for i in range(1, GROUPS + 2):
             for b in range(4):
-                second_matmul(i - 1, b)
-            for b in range(4):
+                first_matmul(i, b)
                 relu_out(i, b)
+                if b == 1:
+                    transpose_back(i - 2, 2)
+            if i == 1:
+                quantise_hidden(0, 1)
+            slot(4 * (i - 2) + 1)
             regroup_hidden(i, 0)
-            relu_out(i, 4)
-            mean_var(i - 2, 2)
-            mean_var(i - 2, 3)
-            centre_gain(i - 2, 2)
-            centre_gain(i - 2, 3)
-            bias_out(i - 1, 0)
-            one_over_std(i - 2)
-            for b in range(1, 4):
-                bias_out(i - 1, b)
-            for j in range(TILES):
-                scale_shift_store(i - 2, j)
             transpose_in(i + 1, 0)
             transpose_in(i + 1, 1)
             copy_in(i + 1, 0)
             copy_in(i + 1, 1)
+            one_over_std(i - 2, 0)
+            for b in range(4, 6):
+                first_matmul(i, b)
+                relu_out(i, b)
+            if i > 1:
+                quantise_hidden(i - 1, 1)
+            slot(4 * (i - 2) + 2)
+            transpose_back(i - 2, 3)
+            for b in range(4):
+                second_matmul(i - 1, b)
+                bias_out(i - 1, b)
+            slot(4 * (i - 2) + 3)
+            for b in range(6, 8):
+                first_matmul(i, b)
+                relu_out(i, b)
             quantise_hidden(i, 0)
             quantise_h(i + 1)
-            if i == -1:
-                regroup_w1(1, nc.vector.tensor_copy)
-                quantise_w1(1)
-                regroup_w2(0)
-                regroup_w2(1)
-                quantise_w2(0)
-                quantise_w2(1)
-            for b in range(5, 8):
-                first_matmul(i, b)
-            for b in range(5, 8):
-                relu_out(i, b)
             regroup_hidden(i, 1)
             transpose_back(i - 1, 0)
             transpose_back(i - 1, 1)
-            mean_var(i - 1, 0)
-            centre_gain(i - 1, 0)
-            for b in range(5):
-                first_matmul(i + 1, b)
-            if i == -1:
-                spread_vectors()
-            transpose_back(i - 1, 2)
-            mean_var(i - 1, 1)
-            centre_gain(i - 1, 1)
-            transpose_back(i - 1, 3)
+            one_over_std(i - 2, 1)
+            slot(4 * (i - 1))
+        for n in range(4 * GROUPS + 1, 4 * GROUPS + 4):
+            slot(n)

@@ -23,7 +23,8 @@ TILES = GROUP // P
 GROUPS = TOKENS // GROUP
 BANK = 512
 CHUNK = 256
-OFF = (1,)
+UNITS = (4, 4, 4, 4, 4, 4, 4, 4)
+START = [sum(UNITS[:u]) for u in range(len(UNITS) + 1)]
 
 
 def tile_ffnn_encoder_pc_t_kernel(tc, h_attn, W1, b1, W2, b2, g2, beta2, out):
@@ -43,6 +44,8 @@ def tile_ffnn_encoder_pc_t_kernel(tc, h_attn, W1, b1, W2, b2, g2, beta2, out):
             k = ring_next[ring] % ring_size[ring]
             ring_next[ring] += 1
             return psum.tile([P, cols], dtype, tag="%s%d" % (ring, k), name="%s%d" % (ring, k))
+
+        live = {}
 
         rows = keep.tile([P, 2 * D], BF16)
         nc.vector.memset(rows[:], 0.0)
@@ -66,7 +69,7 @@ def tile_ffnn_encoder_pc_t_kernel(tc, h_attn, W1, b1, W2, b2, g2, beta2, out):
         nc.scalar.activation(out=warm[:], in_=eps_t[:], func=ACT.Abs_reciprocal_sqrt)
 
         h_sb = [keep.tile([P, TILES * D], BF16, name="h%d" % g) for g in range(GROUPS)]
-        w1raw = keep.tile([P, 4, F], BF16)
+        w1raw = [keep.tile([P, 4, F // 2], BF16, name="w1raw%d" % half) for half in range(2)]
         w2raw = keep.tile([P, 2, 4, D], BF16)
 
         def load_h(g):
@@ -78,14 +81,19 @@ def tile_ffnn_encoder_pc_t_kernel(tc, h_attn, W1, b1, W2, b2, g2, beta2, out):
         def load_w1(half):
             for u in range(2):
                 nc.sync.dma_start(
-                    out=w1raw[:, 2 * u:2 * u + 2, half * 512:(half + 1) * 512],
+                    out=w1raw[half][:, 2 * u:2 * u + 2, :],
                     in_=W1[256 * u:256 * u + 256, half * 512:(half + 1) * 512].rearrange(
                         "(q e) f -> q e f", e=2
                     ),
                 )
 
-        load_h(0)
-        load_w1(0)
+        for pair in range(2):
+            nc.sync.dma_start(
+                out=h_sb[0][:, pair * 2 * D:(pair + 1) * 2 * D],
+                in_=h[0:GROUP, :].rearrange("(p j) d -> p (j d)", j=TILES)[:, pair * 2 * D:(pair + 1) * 2 * D],
+            )
+            if pair == 0:
+                load_w1(0)
         load_w1(1)
         for half in range(2):
             nc.sync.dma_start(
@@ -103,13 +111,15 @@ def tile_ffnn_encoder_pc_t_kernel(tc, h_attn, W1, b1, W2, b2, g2, beta2, out):
 
         def spread_vectors():
             nc.tensor.matmul(out=beta2_bc[:], lhsT=ones[:], rhs=rows[:, D:2 * D], start=True, stop=True)
-            g2_ps = next_bank("v")
-            nc.tensor.matmul(out=g2_ps[:], lhsT=ones[:], rhs=rows[:, 0:D], start=True, stop=True)
-            nc.vector.tensor_copy(out=g2_bc[:], in_=g2_ps[:])
-            nc.scalar.copy(out=beta2_sb[:], in_=beta2_bc[:])
-            b2_ps = next_bank("v", BF16, P)
-            nc.tensor.transpose(b2_ps[:], b2rows[:], identb[:])
-            nc.vector.tensor_copy(out=b2f[:], in_=b2_ps[:, 0:4])
+            live["g2"] = next_bank("v")
+            nc.tensor.matmul(out=live["g2"][:], lhsT=ones[:], rhs=rows[:, 0:D], start=True, stop=True)
+            live["b2"] = next_bank("v", BF16, P)
+            nc.tensor.transpose(live["b2"][:], b2rows[:], identb[:])
+
+        def keep_vectors():
+            nc.vector.tensor_copy(out=b1f[:], in_=b1raw[:].rearrange("p g t -> p (g t)"))
+            nc.vector.tensor_copy(out=g2_bc[:], in_=live["g2"][:])
+            nc.vector.tensor_copy(out=b2f[:], in_=live["b2"][:, 0:4])
 
         def regroup(engine, out, in_):
             if engine == "gpsimd":
@@ -131,7 +141,7 @@ def tile_ffnn_encoder_pc_t_kernel(tc, h_attn, W1, b1, W2, b2, g2, beta2, out):
             regroup(
                 engine,
                 w1g[:, block * 512:(block + 1) * 512].rearrange("q (p t) -> q p t", t=4),
-                w1raw[:, :, half * 512:(half + 1) * 512].rearrange("q t (p s) -> q s p t", s=4)[:, s],
+                w1raw[half][:].rearrange("q t (p s) -> q s p t", s=4)[:, s],
             )
 
         def quantise_w1(half):
@@ -156,291 +166,401 @@ def tile_ffnn_encoder_pc_t_kernel(tc, h_attn, W1, b1, W2, b2, g2, beta2, out):
                 in_=w2g[:, half * 2048:(half + 1) * 2048],
             )
 
-        live = {}
 
-        def absent(g):
-            return g < 0 or g >= GROUPS
+        def absent(u):
+            return u < 0 or u >= len(UNITS)
 
-        def transpose_in(g, half):
-            if absent(g):
+        def tokens(u):
+            return UNITS[u] * P
+
+        def h_tile(n):
+            return h_sb[n // TILES][:, (n % TILES) * D:(n % TILES + 1) * D]
+
+        def transpose_in(u, pair):
+            if absent(u) or 2 * pair >= UNITS[u]:
                 return
-            words = h_sb[g][:].bitcast(F32)
             xt = next_bank("s")
-            live[("xt", g, half)] = xt
+            live[("xt", u, pair)] = xt
             for jl in range(2):
-                j = 2 * half + jl
-                for u in range(2):
+                words = h_tile(START[u] + 2 * pair + jl).bitcast(F32)
+                for k in range(2):
                     nc.tensor.transpose(
-                        xt[:, u * 256 + jl * 128:u * 256 + jl * 128 + 128],
-                        words[:, j * 256 + u * 128:j * 256 + u * 128 + 128],
+                        xt[:, k * 256 + jl * 128:k * 256 + jl * 128 + 128],
+                        words[:, k * 128:k * 128 + 128],
                         ident[:],
                     )
 
-        def copy_in(g, half):
-            if absent(g):
+        def copy_in(u, pair):
+            if absent(u) or 2 * pair >= UNITS[u]:
                 return
-            if half == 0:
-                live[("hg", g)] = work.tile([P, 4 * GROUP], BF16, align_bytes=64, tag="hg", name="hg", bufs=2)
-            pairs = live[("hg", g)][:].bitcast(F32).rearrange("q (c u) -> q c u", u=2)
+            if pair == 0:
+                live[("hg", u)] = work.tile([P, 4 * GROUP], BF16, align_bytes=64, tag="hg", name="hg", bufs=2)
+            pairs = live[("hg", u)][:].bitcast(F32).rearrange("q (c k) -> q c k", k=2)
             nc.scalar.copy(
-                out=pairs[:, half * 256:(half + 1) * 256, :],
-                in_=live[("xt", g, half)][:].rearrange("q (u c) -> q c u", u=2),
+                out=pairs[:, pair * 256:(pair + 1) * 256, :],
+                in_=live[("xt", u, pair)][:].rearrange("q (k c) -> q c k", k=2),
             )
 
-        def quantise_h(g):
-            if absent(g):
+        def quantise_h(u):
+            if absent(u):
                 return
             hc = work.tile([P, GROUP], U32, align_bytes=64, tag="hc", name="hc", bufs=3)
             hs = work.tile([P, GROUP], U8, align_bytes=64, tag="hs", name="hs", bufs=3)
-            live[("hc", g)] = (hc, hs)
-            nc.vector.quantize_mx(out=hc[:].bitcast(FP8X4), scales=hs[:], in_=live[("hg", g)][:])
+            live[("hc", u)] = (hc, hs)
+            c = tokens(u)
+            nc.vector.quantize_mx(out=hc[:, 0:c].bitcast(FP8X4), scales=hs[:, 0:c], in_=live[("hg", u)][:, 0:4 * c])
 
-        def first_matmul(g, b, ring="s"):
-            if absent(g):
+        def first_matmul(u, b, ring="s"):
+            if absent(u):
                 return
-            hc, hs = live[("hc", g)]
+            hc, hs = live[("hc", u)]
             hp = next_bank(ring)
-            live[("hp", g, b)] = hp
+            live[("hp", u, b)] = hp
+            c = tokens(u)
             nc.tensor.matmul_mx(
-                out=hp[:],
+                out=hp[:, 0:c],
                 lhsT=w1c[:, b * 128:(b + 1) * 128].bitcast(FP8X4),
                 lhsT_scale=w1s[:, b * 128:(b + 1) * 128],
-                rhs=hc[:].bitcast(FP8X4),
-                rhs_scale=hs[:],
+                rhs=hc[:, 0:c].bitcast(FP8X4),
+                rhs_scale=hs[:, 0:c],
                 start=True,
                 stop=True,
             )
 
-        def relu_out(g, b, engine="scalar"):
-            if absent(g):
+        def relu_out(u, b, engine="scalar"):
+            if absent(u):
                 return
             if b % 4 == 0:
-                live[("planes", g, b // 4)] = work.tile([P, 4, GROUP], BF16, tag="planes", name="planes", bufs=3)
-            out = live[("planes", g, b // 4)][:, b % 4, :]
+                live[("planes", u, b // 4)] = work.tile([P, 4, GROUP], BF16, tag="planes", name="planes", bufs=4)
+            c = tokens(u)
+            out = live[("planes", u, b // 4)][:, b % 4, 0:c]
             if engine == "scalar":
                 nc.scalar.activation(
-                    out=out, in_=live[("hp", g, b)][:], func=ACT.Relu, bias=b1f[:, b:b + 1], scale=1.0,
+                    out=out, in_=live[("hp", u, b)][:, 0:c], func=ACT.Relu, bias=b1f[:, b:b + 1], scale=1.0,
                 )
             else:
                 nc.vector.tensor_scalar(
-                    out=out, in0=live[("hp", g, b)][:], scalar1=b1f[:, b:b + 1], scalar2=0.0,
+                    out=out, in0=live[("hp", u, b)][:, 0:c], scalar1=b1f[:, b:b + 1], scalar2=0.0,
                     op0=ALU.add, op1=ALU.max,
                 )
 
-        def regroup_hidden(g, half, engine="gpsimd", lo=0, hi=GROUP):
-            if absent(g):
+        def regroup_hidden(u, half, engine="gpsimd"):
+            if absent(u):
                 return
-            if lo == 0:
-                live[("hid_g", g, half)] = work.tile([P, 4 * GROUP], BF16, align_bytes=64, tag="hid_g", name="hid_g", bufs=2)
+            hid_g = work.tile([P, 4 * GROUP], BF16, align_bytes=64, tag="hid_g", name="hid_g", bufs=2)
+            live[("hid_g", u, half)] = hid_g
+            planes = live[("planes", u, half)]
             if engine == "gpsimd":
-                for c in range(lo, hi, CHUNK):
+                for c in range(0, tokens(u), CHUNK):
                     regroup(
                         engine,
-                        live[("hid_g", g, half)][:, 4 * c:4 * (c + CHUNK)].rearrange("p (c t) -> p c t", t=4),
-                        live[("planes", g, half)][:, :, c:c + CHUNK].rearrange("p t c -> p c t"),
+                        hid_g[:, 4 * c:4 * (c + CHUNK)].rearrange("p (c t) -> p c t", t=4),
+                        planes[:, :, c:c + CHUNK].rearrange("p t c -> p c t"),
                     )
             else:
+                c = tokens(u)
                 regroup(
                     engine,
-                    live[("hid_g", g, half)][:, 4 * lo:4 * hi].rearrange("p (c i t) -> p c t i", i=4, t=4),
-                    live[("planes", g, half)][:, :, lo:hi].rearrange("p t (c i) -> p c t i", i=4),
+                    hid_g[:, 0:4 * c].rearrange("p (c i t) -> p c t i", i=4, t=4),
+                    planes[:, :, 0:c].rearrange("p t (c i) -> p c t i", i=4),
                 )
 
-        def quantise_hidden(g, half):
-            if absent(g):
+        def quantise_hidden(u, half):
+            if absent(u):
                 return
             hid_c = work.tile([P, GROUP], U32, align_bytes=64, tag="hid_c", name="hid_c", bufs=4)
             hid_s = work.tile([P, GROUP], U8, align_bytes=64, tag="hid_s", name="hid_s", bufs=4)
-            live[("hid_c", g, half)] = (hid_c, hid_s)
-            nc.vector.quantize_mx(out=hid_c[:].bitcast(FP8X4), scales=hid_s[:], in_=live[("hid_g", g, half)][:])
+            live[("hid_c", u, half)] = (hid_c, hid_s)
+            c = tokens(u)
+            nc.vector.quantize_mx(
+                out=hid_c[:, 0:c].bitcast(FP8X4), scales=hid_s[:, 0:c], in_=live[("hid_g", u, half)][:, 0:4 * c]
+            )
 
-        def second_matmul(g, b):
-            if absent(g):
+        def second_matmul(u, b):
+            if absent(u):
                 return
             ft = next_bank("s")
-            live[("ft", g, b)] = ft
+            live[("ft", u, b)] = ft
+            c = tokens(u)
             for half in range(2):
-                hid_c, hid_s = live[("hid_c", g, half)]
+                hid_c, hid_s = live[("hid_c", u, half)]
                 nc.tensor.matmul_mx(
-                    out=ft[:],
+                    out=ft[:, 0:c],
                     lhsT=w2c[:, half * D + b * 128:half * D + (b + 1) * 128].bitcast(FP8X4),
                     lhsT_scale=w2s[:, half * D + b * 128:half * D + (b + 1) * 128],
-                    rhs=hid_c[:].bitcast(FP8X4),
-                    rhs_scale=hid_s[:],
+                    rhs=hid_c[:, 0:c].bitcast(FP8X4),
+                    rhs_scale=hid_s[:, 0:c],
                     start=(half == 0),
                     stop=(half == 1),
                 )
 
-        def bias_out(g, b):
-            if absent(g):
+        def bias_out(u, b):
+            if absent(u):
                 return
             if b == 0:
-                live[("x_t", g)] = work.tile([P, 4, GROUP], F32, tag="x_t", name="x_t", bufs=2)
+                live[("x_t", u)] = work.tile([P, 4, GROUP], F32, tag="x_t", name="x_t", bufs=2)
+            c = tokens(u)
             nc.scalar.activation(
-                out=live[("x_t", g)][:, b, :], in_=live[("ft", g, b)][:],
+                out=live[("x_t", u)][:, b, 0:c], in_=live[("ft", u, b)][:, 0:c],
                 func=ACT.Identity, bias=b2f[:, b:b + 1], scale=1.0,
             )
 
-        def transpose_back(g, j):
-            if absent(g):
+        def tile_of(u, j):
+            return None if absent(u) or j >= UNITS[u] else START[u] + j
+
+        def transpose_back(u, j):
+            n = tile_of(u, j)
+            if n is None:
                 return
             xb = next_bank("v")
-            live[("xb", g, j)] = xb
-            nc.tensor.matmul(out=xb[:], lhsT=identb[:], rhs=h_sb[g][:, j * D:(j + 1) * D], start=True, stop=False)
+            live[("xb", n)] = xb
+            nc.tensor.matmul(out=xb[:], lhsT=identb[:], rhs=h_tile(n), start=True, stop=False)
             for b in range(4):
                 nc.tensor.matmul(
                     out=xb[:, b * 128:(b + 1) * 128],
-                    lhsT=live[("x_t", g)][:, b, j * 128:(j + 1) * 128],
+                    lhsT=live[("x_t", u)][:, b, j * 128:(j + 1) * 128],
                     rhs=ident[:],
                     is_transpose=True,
                     start=False,
                     stop=(b == 3),
                 )
 
+        def outside(n):
+            return n is None or n < 0 or n >= START[-1]
+
         def stats(n):
-            g, j = divmod(n, TILES)
-            if absent(g):
+            if outside(n):
                 return
-            if j == 0:
-                live[("mv", g)] = work.tile([P, TILES, 2], F32, tag="mv", name="mv", bufs=3)
             st = work.tile([P, 6], F32, tag="st", name="st", bufs=6)
             live[("st", n)] = st
-            nc.vector.bn_stats(out=st[:], in_=live[("xb", g, j)][:])
+            nc.vector.bn_stats(out=st[:], in_=live[("xb", n)][:])
 
         def aggregate(n):
-            g, j = divmod(n, TILES)
-            if absent(g):
+            if outside(n):
                 return
-            nc.vector.bn_aggr(out=live[("mv", g)][:, j, :], in_=live[("st", n)][:])
+            if n % 2 == 0:
+                live[("mv", n // 2)] = work.tile([P, 2, 2], F32, tag="mv", name="mv", bufs=6)
+            nc.vector.bn_aggr(out=live[("mv", n // 2)][:, n % 2, :], in_=live[("st", n)][:])
 
         def centre_gain(n):
-            g, j = divmod(n, TILES)
-            if absent(g):
+            if outside(n):
                 return
             t1 = work.tile([P, D], F32, tag="t1", name="t1", bufs=8)
             live[("t1", n)] = t1
             nc.vector.scalar_tensor_tensor(
-                out=t1[:], in0=live[("xb", g, j)][:], scalar=live[("mv", g)][:, j, 0:1], in1=g2_bc[:],
+                out=t1[:], in0=live[("xb", n)][:], scalar=live[("mv", n // 2)][:, n % 2, 0:1], in1=g2_bc[:],
                 op0=ALU.subtract, op1=ALU.mult,
             )
 
-        def one_over_std(g, half):
-            if absent(g):
+        def one_over_std(n):
+            if outside(n):
                 return
             rstd = work.tile([P, 2], F32, tag="rstd", name="rstd", bufs=6)
-            live[("rstd", g, half)] = rstd
+            live[("rstd", n // 2)] = rstd
             nc.scalar.activation(
-                out=rstd[:], in_=live[("mv", g)][:, 2 * half:2 * half + 2, 1], func=ACT.Abs_reciprocal_sqrt,
+                out=rstd[:], in_=live[("mv", n // 2)][:, :, 1], func=ACT.Abs_reciprocal_sqrt,
                 bias=eps_t[:, 0:1], scale=1.0,
             )
 
         def scale(n):
-            g, j = divmod(n, TILES)
-            if absent(g):
+            if outside(n):
                 return
-            t2 = work.tile([P, D], F32, tag="t2", name="t2", bufs=4)
+            t2 = work.tile([P, D], F32, tag="t2", name="t2", bufs=6)
             live[("t2", n)] = t2
             nc.scalar.activation(
-                out=t2[:], in_=live[("t1", n)][:], func=ACT.Copy, scale=live[("rstd", g, j // 2)][:, j % 2:j % 2 + 1],
+                out=t2[:], in_=live[("t1", n)][:], func=ACT.Copy, scale=live[("rstd", n // 2)][:, n % 2:n % 2 + 1],
             )
 
-        def scale_shift_store(n):
-            g, j = divmod(n, TILES)
-            if absent(g):
+        def shift_store(n):
+            if outside(n):
                 return
-            if j % 2 == 0:
-                live[("ot", g)] = work.tile([P, 2 * D], F32, tag="ot", name="ot", bufs=4)
-            ot = live[("ot", g)]
+            pair, half = divmod(n, 2)
+            first = ("ot", pair) not in live
+            if first:
+                live[("ot", pair)] = work.tile([P, 2 * D], F32, tag="ot", name="ot", bufs=7)
+            ot = live[("ot", pair)]
+            out = ot[:, half * D:(half + 1) * D]
             if ("t2", n) in live:
-                nc.gpsimd.tensor_tensor(out=ot[:, (j % 2) * D:(j % 2 + 1) * D], in0=live[("t2", n)][:], in1=beta2_sb[:], op=ALU.add)
+                nc.gpsimd.tensor_tensor(out=out, in0=live[("t2", n)][:], in1=beta2_sb[:], op=ALU.add)
             else:
                 nc.vector.scalar_tensor_tensor(
-                    out=ot[:, (j % 2) * D:(j % 2 + 1) * D], in0=live[("t1", n)][:],
-                    scalar=live[("rstd", g, j // 2)][:, j % 2:j % 2 + 1], in1=beta2_bc[:], op0=ALU.mult, op1=ALU.add,
+                    out=out, in0=live[("t1", n)][:], scalar=live[("rstd", pair)][:, half:half + 1], in1=beta2_bc[:],
+                    op0=ALU.mult, op1=ALU.add,
                 )
-            if j % 2 == 1:
+            if not first:
+                g, j = divmod(2 * pair, TILES)
                 nc.sync.dma_start(
-                    out=o[g * GROUP:(g + 1) * GROUP, :].rearrange("(p j) d -> p j d", j=TILES)[:, j - 1:j + 1, :],
+                    out=o[g * GROUP:(g + 1) * GROUP, :].rearrange("(p j) d -> p j d", j=TILES)[:, j:j + 2, :],
                     in_=ot[:].rearrange("p (j d) -> p j d", j=2),
                 )
 
-        def slot(n, lag=4):
-            stats(n)
-            centre_gain(n - 1)
-            aggregate(n)
-            scale_shift_store(n - lag)
-
         transpose_in(0, 0)
-        transpose_in(0, 1)
         copy_in(0, 0)
-        copy_in(0, 1)
         spread_vectors()
-        nc.vector.tensor_copy(out=b1f[:], in_=b1raw[:].rearrange("p g t -> p (g t)"))
+        transpose_in(0, 1)
+        for s in range(4):
+            regroup_w1(0, s, "vector" if s < 2 else "scalar")
+        copy_in(0, 1)
+        quantise_w1(0)
+        for s in range(4):
+            regroup_w1(1, s, "vector" if s < 2 else "scalar")
         quantise_h(0)
-        for half in range(2):
-            for s in range(3):
-                regroup_w1(half, s, "vector")
-            regroup_w1(half, 3, "scalar")
-            if half == 0:
-                quantise_w1(half)
-        regroup_w2(0, 0, "scalar")
-        for b in range(4):
-            first_matmul(0, b, "sv"[b % 2])
-        for b in range(4):
-            relu_out(0, b, ("scalar", "vector")[b % 2])
-        regroup_w2(1, 0, "gpsimd")
-        quantise_w1(1)
-        regroup_hidden(0, 0, "vector")
+        keep_vectors()
+        first_matmul(0, 0)
+        first_matmul(0, 1, "v")
+        first_matmul(0, 2)
+        first_matmul(0, 3, "v")
         transpose_in(1, 0)
         transpose_in(1, 1)
+        quantise_w1(1)
+        relu_out(0, 0)
+        relu_out(0, 1, "vector")
+        relu_out(0, 2)
+        relu_out(0, 3, "vector")
+        copy_in(1, 0)
+        copy_in(1, 1)
+        regroup_w2(0, 0, "gpsimd")
+        regroup_w2(0, 1, "scalar")
         for b in range(4, 8):
-            first_matmul(0, b)
-            relu_out(0, b)
-            if b == 5:
-                copy_in(1, 0)
-                copy_in(1, 1)
-        regroup_w2(0, 1, "vector")
-        quantise_hidden(0, 0)
+            first_matmul(0, b, "v" if b == 7 else "s")
+        relu_out(0, 4)
+        relu_out(0, 7, "vector")
+        relu_out(0, 5)
+        relu_out(0, 6)
+        regroup_hidden(0, 0, "vector")
         quantise_h(1)
-        regroup_w2(1, 1, "gpsimd")
-        regroup_hidden(0, 1, "vector")
+        quantise_hidden(0, 0)
+        regroup_w2(1, 0, "scalar")
         quantise_w2(0)
+        regroup_hidden(0, 1, "vector")
+        regroup_w2(1, 1, "vector")
+        quantise_hidden(0, 1)
         quantise_w2(1)
-        for i in range(1, GROUPS + 2):
-            for b in range(4):
-                first_matmul(i, b)
-                relu_out(i, b)
-                if b == 1:
-                    transpose_back(i - 2, 2)
-            if i == 1:
-                quantise_hidden(0, 1)
-            slot(4 * (i - 2) + 1)
-            regroup_hidden(i, 0)
-            transpose_in(i + 1, 0)
-            transpose_in(i + 1, 1)
-            copy_in(i + 1, 0)
-            copy_in(i + 1, 1)
-            one_over_std(i - 2, 0)
-            for b in range(4, 6):
-                first_matmul(i, b)
-                relu_out(i, b)
-            if i > 1:
-                quantise_hidden(i - 1, 1)
-            slot(4 * (i - 2) + 2)
-            transpose_back(i - 2, 3)
-            for b in range(4):
-                second_matmul(i - 1, b)
-                bias_out(i - 1, b)
-            slot(4 * (i - 2) + 3)
+        for b in range(4):
+            first_matmul(1, b)
+            relu_out(1, b)
+        transpose_in(2, 0)
+        transpose_in(2, 1)
+        copy_in(2, 0)
+        copy_in(2, 1)
+        for b in range(4):
+            second_matmul(0, b)
+            bias_out(0, b)
+        nc.scalar.copy(out=beta2_sb[:], in_=beta2_bc[:])
+        quantise_h(2)
+        regroup_hidden(1, 0, "vector")
+        for b in range(4, 8):
+            first_matmul(1, b, "v" if b % 2 else "s")
+        for b in range(4, 8):
+            relu_out(1, b, "vector" if b % 2 else "scalar")
+        regroup_hidden(1, 1)
+        for u in range(2, len(UNITS)):
+            n = 4 * (u - 2)
+            first_matmul(u, 0)
+            relu_out(u, 0)
+            transpose_in(u + 1, 0)
+            quantise_hidden(u - 1, 0)
+            centre_gain(n - 1)
+            transpose_back(u - 2, 0)
+            stats(n)
+            first_matmul(u, 1)
+            first_matmul(u, 2)
+            relu_out(u, 1)
+            copy_in(u + 1, 0)
+            transpose_back(u - 2, 1)
+            shift_store(n - 2)
+            aggregate(n)
+            stats(n + 1)
+            centre_gain(n)
+            first_matmul(u, 4)
+            first_matmul(u, 3)
+            relu_out(u, 2)
+            relu_out(u, 4)
+            quantise_hidden(u - 1, 1)
+            transpose_in(u + 1, 1)
+            copy_in(u + 1, 1)
+            quantise_h(u + 1)
+            relu_out(u, 3)
+            regroup_hidden(u, 0)
+            scale(n - 1)
+            shift_store(n - 1)
+            transpose_back(u - 2, 2)
+            stats(n + 2)
+            aggregate(n + 1)
+            shift_store(n - 4)
+            aggregate(n + 2)
+            centre_gain(n + 1)
+            transpose_back(u - 2, 3)
+            stats(n + 3)
+            centre_gain(n + 2)
+            shift_store(n - 3)
+            aggregate(n + 3)
+            second_matmul(u - 1, 0)
+            bias_out(u - 1, 0)
+            first_matmul(u, 5)
+            relu_out(u, 5)
+            for b in range(1, 4):
+                second_matmul(u - 1, b)
+                bias_out(u - 1, b)
             for b in range(6, 8):
-                first_matmul(i, b)
-                relu_out(i, b)
-            quantise_hidden(i, 0)
-            quantise_h(i + 1)
-            regroup_hidden(i, 1)
-            transpose_back(i - 1, 0)
-            transpose_back(i - 1, 1)
-            one_over_std(i - 2, 1)
-            slot(4 * (i - 1))
-        for n in range(4 * GROUPS + 1, 4 * GROUPS + 4):
-            slot(n)
+                first_matmul(u, b)
+                relu_out(u, b)
+            regroup_hidden(u, 1)
+            one_over_std(n)
+            one_over_std(n + 2)
+        u = len(UNITS)
+        n = 4 * (u - 2)
+        quantise_hidden(u - 1, 0)
+        centre_gain(n - 1)
+        transpose_back(u - 2, 0)
+        stats(n)
+        transpose_back(u - 2, 1)
+        shift_store(n - 2)
+        aggregate(n)
+        stats(n + 1)
+        centre_gain(n)
+        transpose_back(u - 2, 2)
+        aggregate(n + 1)
+        one_over_std(n)
+        stats(n + 2)
+        quantise_hidden(u - 1, 1)
+        centre_gain(n + 1)
+        transpose_back(u - 2, 3)
+        for b in range(4):
+            second_matmul(u - 1, b)
+            bias_out(u - 1, b)
+            if b == 0:
+                scale(n - 1)
+                scale(n)
+        shift_store(n - 1)
+        shift_store(n)
+        aggregate(n + 2)
+        shift_store(n - 4)
+        stats(n + 3)
+        centre_gain(n + 2)
+        shift_store(n - 3)
+        aggregate(n + 3)
+        scale(n + 1)
+        one_over_std(n + 2)
+        shift_store(n + 1)
+        centre_gain(n + 3)
+        scale(n + 2)
+        scale(n + 3)
+        shift_store(n + 2)
+        shift_store(n + 3)
+        n += 4
+        for j in range(4):
+            transpose_back(u - 1, j)
+            stats(n + j)
+            if j > 0:
+                centre_gain(n + j - 1)
+            aggregate(n + j)
+            if j % 2 == 1:
+                one_over_std(n + j - 1)
+            if j == 2:
+                scale(n)
+                shift_store(n)
+        centre_gain(n + 3)
+        shift_store(n + 1)
+        shift_store(n + 2)
+        shift_store(n + 3)

@@ -308,16 +308,21 @@ def tile_ffnn_encoder_pc_t_kernel(tc, h_attn, W1, b1, W2, b2, g2, beta2, out):
         def tile_of(u, j):
             return None if absent(u) or j >= UNITS[u] else START[u] + j
 
-        def transpose_back(u, j):
+        def residual(u, j):
             n = tile_of(u, j)
             if n is None:
                 return
             xb = next_bank("v")
             live[("xb", n)] = xb
             nc.tensor.matmul(out=xb[:], lhsT=identb[:], rhs=h_tile(n), start=True, stop=False)
+
+        def transpose_back(u, j):
+            n = tile_of(u, j)
+            if n is None:
+                return
             for b in range(4):
                 nc.tensor.matmul(
-                    out=xb[:, b * 128:(b + 1) * 128],
+                    out=live[("xb", n)][:, b * 128:(b + 1) * 128],
                     lhsT=live[("x_t", u)][:, b, j * 128:(j + 1) * 128],
                     rhs=ident[:],
                     is_transpose=True,
@@ -453,27 +458,30 @@ def tile_ffnn_encoder_pc_t_kernel(tc, h_attn, W1, b1, W2, b2, g2, beta2, out):
             first_matmul(1, b, "v" if b % 2 else "s")
         for b in range(4, 8):
             relu_out(1, b, "vector" if b % 2 else "scalar")
+        residual(0, 0)
+        residual(0, 1)
         regroup_hidden(1, 1)
         for u in range(2, len(UNITS)):
             n = 4 * (u - 2)
             first_matmul(u, 0)
             relu_out(u, 0)
+            first_matmul(u, 1)
+            relu_out(u, 1)
             transpose_in(u + 1, 0)
             quantise_hidden(u - 1, 0)
             centre_gain(n - 1)
             transpose_back(u - 2, 0)
             stats(n)
-            first_matmul(u, 1)
-            first_matmul(u, 2)
-            relu_out(u, 1)
-            copy_in(u + 1, 0)
             transpose_back(u - 2, 1)
+            first_matmul(u, 2)
+            copy_in(u + 1, 0)
             shift_store(n - 2)
             aggregate(n)
             stats(n + 1)
             centre_gain(n)
             first_matmul(u, 4)
             first_matmul(u, 3)
+            residual(u - 2, 2)
             relu_out(u, 2)
             relu_out(u, 4)
             quantise_hidden(u - 1, 1)
@@ -490,6 +498,7 @@ def tile_ffnn_encoder_pc_t_kernel(tc, h_attn, W1, b1, W2, b2, g2, beta2, out):
             shift_store(n - 4)
             aggregate(n + 2)
             centre_gain(n + 1)
+            residual(u - 2, 3)
             transpose_back(u - 2, 3)
             stats(n + 3)
             centre_gain(n + 2)
@@ -505,6 +514,8 @@ def tile_ffnn_encoder_pc_t_kernel(tc, h_attn, W1, b1, W2, b2, g2, beta2, out):
             for b in range(6, 8):
                 first_matmul(u, b)
                 relu_out(u, b)
+            residual(u - 1, 0)
+            residual(u - 1, 1)
             regroup_hidden(u, 1)
             one_over_std(n)
             one_over_std(n + 2)
@@ -519,12 +530,14 @@ def tile_ffnn_encoder_pc_t_kernel(tc, h_attn, W1, b1, W2, b2, g2, beta2, out):
         aggregate(n)
         stats(n + 1)
         centre_gain(n)
+        residual(u - 2, 2)
         transpose_back(u - 2, 2)
         aggregate(n + 1)
         one_over_std(n)
         stats(n + 2)
         quantise_hidden(u - 1, 1)
         centre_gain(n + 1)
+        residual(u - 2, 3)
         transpose_back(u - 2, 3)
         for b in range(4):
             second_matmul(u - 1, b)
@@ -550,6 +563,7 @@ def tile_ffnn_encoder_pc_t_kernel(tc, h_attn, W1, b1, W2, b2, g2, beta2, out):
         shift_store(n + 3)
         n += 4
         for j in range(4):
+            residual(u - 1, j)
             transpose_back(u - 1, j)
             stats(n + j)
             if j > 0:

@@ -22,7 +22,7 @@ GROUP = 512
 TILES = GROUP // P
 GROUPS = TOKENS // GROUP
 BANK = 512
-CHUNK = 256
+CHUNK = 512
 UNITS = (4, 4, 4, 4, 4, 4, 4, 4)
 START = [sum(UNITS[:u]) for u in range(len(UNITS) + 1)]
 
@@ -490,7 +490,6 @@ def tile_ffnn_encoder_pc_t_kernel(tc, h_attn, W1, b1, W2, b2, g2, beta2, out):
             quantise_h(u + 1)
             relu_out(u, 3)
             regroup_hidden(u, 0)
-            scale(n - 1)
             shift_store(n - 1)
             transpose_back(u - 2, 2)
             stats(n + 2)

@@ -22,7 +22,6 @@ GROUP = 512
 TILES = GROUP // P
 GROUPS = TOKENS // GROUP
 BANK = 512
-CHUNK = 512
 UNITS = (4, 4, 4, 4, 4, 4, 4, 4)
 START = [sum(UNITS[:u]) for u in range(len(UNITS) + 1)]
 
@@ -92,15 +91,14 @@ def tile_ffnn_encoder_pc_t_kernel(tc, h_attn, W1, b1, W2, b2, g2, beta2, out):
                 out=h_sb[0][:, pair * 2 * D:(pair + 1) * 2 * D],
                 in_=h[0:GROUP, :].rearrange("(p j) d -> p (j d)", j=TILES)[:, pair * 2 * D:(pair + 1) * 2 * D],
             )
-            if pair == 0:
-                load_w1(0)
-        load_w1(1)
+            load_w1(pair)
         for half in range(2):
             nc.sync.dma_start(
                 out=w2raw[:, half],
                 in_=W2[512 * half:512 * half + 512, :].rearrange("(p t) d -> p t d", t=4),
             )
-        for g in range(1, GROUPS):
+            load_h(half + 1)
+        for g in range(3, GROUPS):
             load_h(g)
 
         b1f = keep.tile([P, 8], F32)
@@ -230,7 +228,7 @@ def tile_ffnn_encoder_pc_t_kernel(tc, h_attn, W1, b1, W2, b2, g2, beta2, out):
         def relu_out(u, b, engine="scalar"):
             if absent(u):
                 return
-            if b % 4 == 0:
+            if ("planes", u, b // 4) not in live:
                 live[("planes", u, b // 4)] = work.tile([P, 4, GROUP], BF16, tag="planes", name="planes", bufs=4)
             c = tokens(u)
             out = live[("planes", u, b // 4)][:, b % 4, 0:c]
@@ -247,22 +245,23 @@ def tile_ffnn_encoder_pc_t_kernel(tc, h_attn, W1, b1, W2, b2, g2, beta2, out):
         def regroup_hidden(u, half, engine="gpsimd"):
             if absent(u):
                 return
-            hid_g = work.tile([P, 4 * GROUP], BF16, align_bytes=64, tag="hid_g", name="hid_g", bufs=2)
+            tag, bufs = ("hid_v", 2) if engine == "vector" else ("hid_g", 1)
+            hid_g = work.tile([P, 4 * GROUP], BF16, align_bytes=64, tag=tag, name=tag, bufs=bufs)
             live[("hid_g", u, half)] = hid_g
             planes = live[("planes", u, half)]
-            if engine == "gpsimd":
-                for c in range(0, tokens(u), CHUNK):
-                    regroup(
-                        engine,
-                        hid_g[:, 4 * c:4 * (c + CHUNK)].rearrange("p (c t) -> p c t", t=4),
-                        planes[:, :, c:c + CHUNK].rearrange("p t c -> p c t"),
-                    )
-            else:
-                c = tokens(u)
+            c = tokens(u)
+            cut = {"gpsimd": c, "both": c // 2}.get(engine, 0)
+            if cut:
                 regroup(
-                    engine,
-                    hid_g[:, 0:4 * c].rearrange("p (c i t) -> p c t i", i=4, t=4),
-                    planes[:, :, 0:c].rearrange("p t (c i) -> p c t i", i=4),
+                    "gpsimd",
+                    hid_g[:, 0:4 * cut].rearrange("p (c t) -> p c t", t=4),
+                    planes[:, :, 0:cut].rearrange("p t c -> p c t"),
+                )
+            if cut < c:
+                regroup(
+                    "vector" if engine == "vector" else "scalar",
+                    hid_g[:, 4 * cut:4 * c].rearrange("p (c i t) -> p c t i", i=4, t=4),
+                    planes[:, :, cut:c].rearrange("p t (c i) -> p c t i", i=4),
                 )
 
         def quantise_hidden(u, half):
@@ -276,10 +275,10 @@ def tile_ffnn_encoder_pc_t_kernel(tc, h_attn, W1, b1, W2, b2, g2, beta2, out):
                 out=hid_c[:, 0:c].bitcast(FP8X4), scales=hid_s[:, 0:c], in_=live[("hid_g", u, half)][:, 0:4 * c]
             )
 
-        def second_matmul(u, b):
+        def second_matmul(u, b, ring="s"):
             if absent(u):
                 return
-            ft = next_bank("s")
+            ft = next_bank(ring)
             live[("ft", u, b)] = ft
             c = tokens(u)
             for half in range(2):
@@ -370,7 +369,7 @@ def tile_ffnn_encoder_pc_t_kernel(tc, h_attn, W1, b1, W2, b2, g2, beta2, out):
         def scale(n):
             if outside(n):
                 return
-            t2 = work.tile([P, D], F32, tag="t2", name="t2", bufs=6)
+            t2 = work.tile([P, D], F32, tag="t2", name="t2", bufs=11)
             live[("t2", n)] = t2
             nc.scalar.activation(
                 out=t2[:], in_=live[("t1", n)][:], func=ACT.Copy, scale=live[("rstd", n // 2)][:, n % 2:n % 2 + 1],
@@ -379,25 +378,19 @@ def tile_ffnn_encoder_pc_t_kernel(tc, h_attn, W1, b1, W2, b2, g2, beta2, out):
         def shift_store(n):
             if outside(n):
                 return
-            pair, half = divmod(n, 2)
-            first = ("ot", pair) not in live
-            if first:
-                live[("ot", pair)] = work.tile([P, 2 * D], F32, tag="ot", name="ot", bufs=7)
-            ot = live[("ot", pair)]
-            out = ot[:, half * D:(half + 1) * D]
             if ("t2", n) in live:
-                nc.gpsimd.tensor_tensor(out=out, in0=live[("t2", n)][:], in1=beta2_sb[:], op=ALU.add)
+                ot = live[("t2", n)]
+                nc.gpsimd.tensor_tensor(out=ot[:], in0=ot[:], in1=beta2_sb[:], op=ALU.add)
             else:
+                ot = work.tile([P, D], F32, tag="ot", name="ot", bufs=6)
                 nc.vector.scalar_tensor_tensor(
-                    out=out, in0=live[("t1", n)][:], scalar=live[("rstd", pair)][:, half:half + 1], in1=beta2_bc[:],
-                    op0=ALU.mult, op1=ALU.add,
+                    out=ot[:], in0=live[("t1", n)][:], scalar=live[("rstd", n // 2)][:, n % 2:n % 2 + 1],
+                    in1=beta2_bc[:], op0=ALU.mult, op1=ALU.add,
                 )
-            if not first:
-                g, j = divmod(2 * pair, TILES)
-                nc.sync.dma_start(
-                    out=o[g * GROUP:(g + 1) * GROUP, :].rearrange("(p j) d -> p j d", j=TILES)[:, j:j + 2, :],
-                    in_=ot[:].rearrange("p (j d) -> p j d", j=2),
-                )
+            g, j = divmod(n, TILES)
+            nc.sync.dma_start(
+                out=o[g * GROUP:(g + 1) * GROUP, :].rearrange("(p j) d -> p j d", j=TILES)[:, j, :], in_=ot[:],
+            )
 
         transpose_in(0, 0)
         copy_in(0, 0)
@@ -407,173 +400,183 @@ def tile_ffnn_encoder_pc_t_kernel(tc, h_attn, W1, b1, W2, b2, g2, beta2, out):
             regroup_w1(0, s, "vector" if s < 2 else "scalar")
         copy_in(0, 1)
         quantise_w1(0)
+        quantise_h(0)
         for s in range(4):
             regroup_w1(1, s, "vector" if s < 2 else "scalar")
-        quantise_h(0)
         keep_vectors()
-        first_matmul(0, 0)
-        first_matmul(0, 1, "v")
-        first_matmul(0, 2)
-        first_matmul(0, 3, "v")
+        quantise_w1(1)
+        for b in range(4):
+            first_matmul(0, b, "sv"[b % 2])
         transpose_in(1, 0)
         transpose_in(1, 1)
-        quantise_w1(1)
-        relu_out(0, 0)
-        relu_out(0, 1, "vector")
-        relu_out(0, 2)
-        relu_out(0, 3, "vector")
+        for b in range(4):
+            relu_out(0, b, ("scalar", "vector")[b % 2])
         copy_in(1, 0)
         copy_in(1, 1)
-        regroup_w2(0, 0, "gpsimd")
-        regroup_w2(0, 1, "scalar")
-        for b in range(4, 8):
+        regroup_w2(1, 0, "gpsimd")
+        for b in (7, 4, 5, 6):
             first_matmul(0, b, "v" if b == 7 else "s")
-        relu_out(0, 4)
         relu_out(0, 7, "vector")
-        relu_out(0, 5)
-        relu_out(0, 6)
-        regroup_hidden(0, 0, "vector")
+        for b in range(4, 7):
+            relu_out(0, b)
         quantise_h(1)
-        quantise_hidden(0, 0)
-        regroup_w2(1, 0, "scalar")
-        quantise_w2(0)
+        regroup_hidden(0, 0, "vector")
+        regroup_w2(0, 0, "scalar")
+        regroup_w2(0, 1, "scalar")
         regroup_hidden(0, 1, "vector")
+        quantise_hidden(0, 0)
         regroup_w2(1, 1, "vector")
         quantise_hidden(0, 1)
         quantise_w2(1)
+        quantise_w2(0)
         for b in range(4):
             first_matmul(1, b)
             relu_out(1, b)
+        first_matmul(1, 5, "v")
+        first_matmul(1, 7, "v")
+        relu_out(1, 5, "vector")
+        relu_out(1, 7, "vector")
         transpose_in(2, 0)
         transpose_in(2, 1)
         copy_in(2, 0)
         copy_in(2, 1)
+        quantise_h(2)
         for b in range(4):
             second_matmul(0, b)
             bias_out(0, b)
         nc.scalar.copy(out=beta2_sb[:], in_=beta2_bc[:])
-        quantise_h(2)
         regroup_hidden(1, 0, "vector")
-        for b in range(4, 8):
-            first_matmul(1, b, "v" if b % 2 else "s")
-        for b in range(4, 8):
-            relu_out(1, b, "vector" if b % 2 else "scalar")
         residual(0, 0)
-        residual(0, 1)
+        for b in (4, 6):
+            first_matmul(1, b)
+            relu_out(1, b)
+        quantise_hidden(1, 0)
         regroup_hidden(1, 1)
         for u in range(2, len(UNITS)):
             n = 4 * (u - 2)
+            transpose_in(u + 1, 0)
+            transpose_back(u - 2, 0)
+            copy_in(u + 1, 0)
+            aggregate(n - 1)
+            stats(n)
+            centre_gain(n - 1)
             first_matmul(u, 0)
             relu_out(u, 0)
-            first_matmul(u, 1)
-            relu_out(u, 1)
-            transpose_in(u + 1, 0)
-            quantise_hidden(u - 1, 0)
-            centre_gain(n - 1)
-            transpose_back(u - 2, 0)
-            stats(n)
-            transpose_back(u - 2, 1)
-            first_matmul(u, 2)
-            copy_in(u + 1, 0)
-            shift_store(n - 2)
-            aggregate(n)
-            stats(n + 1)
-            centre_gain(n)
             first_matmul(u, 4)
-            first_matmul(u, 3)
-            residual(u - 2, 2)
-            relu_out(u, 2)
             relu_out(u, 4)
-            quantise_hidden(u - 1, 1)
+            residual(u - 2, 1)
+            transpose_back(u - 2, 1)
             transpose_in(u + 1, 1)
             copy_in(u + 1, 1)
-            quantise_h(u + 1)
-            relu_out(u, 3)
-            regroup_hidden(u, 0)
-            shift_store(n - 1)
-            transpose_back(u - 2, 2)
-            stats(n + 2)
-            aggregate(n + 1)
+            one_over_std(n - 2)
+            aggregate(n)
             shift_store(n - 4)
-            aggregate(n + 2)
+            centre_gain(n)
+            stats(n + 1)
+            for b in range(1, 4):
+                first_matmul(u, b)
+                relu_out(u, b)
+            quantise_hidden(u - 1, 1)
+            quantise_h(u + 1)
+            aggregate(n + 1)
+            regroup_hidden(u, 0)
+            scale(n - 1)
+            shift_store(n - 3)
             centre_gain(n + 1)
+            residual(u - 2, 2)
+            transpose_back(u - 2, 2)
             residual(u - 2, 3)
             transpose_back(u - 2, 3)
-            stats(n + 3)
-            centre_gain(n + 2)
-            shift_store(n - 3)
-            aggregate(n + 3)
-            second_matmul(u - 1, 0)
-            bias_out(u - 1, 0)
-            first_matmul(u, 5)
-            relu_out(u, 5)
-            for b in range(1, 4):
+            stats(n + 2)
+            shift_store(n - 2)
+            aggregate(n + 2)
+            for b in range(5, 6 if u + 1 < len(UNITS) else 8):
+                first_matmul(u, b)
+                relu_out(u, b)
+            for b in range(4):
                 second_matmul(u - 1, b)
                 bias_out(u - 1, b)
-            for b in range(6, 8):
+            stats(n + 3)
+            quantise_hidden(u, 0)
+            centre_gain(n + 2)
+            one_over_std(n)
+            for b in range(6 if u + 1 < len(UNITS) else 8, 8):
                 first_matmul(u, b)
                 relu_out(u, b)
             residual(u - 1, 0)
-            residual(u - 1, 1)
-            regroup_hidden(u, 1)
-            one_over_std(n)
-            one_over_std(n + 2)
+            regroup_hidden(u, 1, "gpsimd" if u + 1 < len(UNITS) else "both")
         u = len(UNITS)
         n = 4 * (u - 2)
-        quantise_hidden(u - 1, 0)
+        aggregate(n - 1)
         centre_gain(n - 1)
+        residual(u - 2, 1)
+        one_over_std(n - 2)
         transpose_back(u - 2, 0)
         stats(n)
         transpose_back(u - 2, 1)
+        scale(n - 2)
+        scale(n - 1)
+        quantise_hidden(u - 1, 1)
         shift_store(n - 2)
         aggregate(n)
-        stats(n + 1)
+        shift_store(n - 4)
+        shift_store(7)
         centre_gain(n)
+        stats(n + 1)
         residual(u - 2, 2)
         transpose_back(u - 2, 2)
         aggregate(n + 1)
-        one_over_std(n)
-        stats(n + 2)
-        quantise_hidden(u - 1, 1)
-        centre_gain(n + 1)
-        residual(u - 2, 3)
-        transpose_back(u - 2, 3)
         for b in range(4):
             second_matmul(u - 1, b)
             bias_out(u - 1, b)
-            if b == 0:
-                scale(n - 1)
-                scale(n)
-        shift_store(n - 1)
-        shift_store(n)
+        shift_store(n - 3)
+        shift_store(11)
+        centre_gain(n + 1)
+        residual(u - 2, 3)
+        transpose_back(u - 2, 3)
+        stats(n + 2)
+        shift_store(15)
         aggregate(n + 2)
-        shift_store(n - 4)
         stats(n + 3)
         centre_gain(n + 2)
-        shift_store(n - 3)
         aggregate(n + 3)
-        scale(n + 1)
+        one_over_std(n)
         one_over_std(n + 2)
-        shift_store(n + 1)
+        for k in (19,):
+            shift_store(k)
+        shift_store(3)
+        residual(u - 1, 0)
+        transpose_back(u - 1, 0)
+        stats(n + 4)
         centre_gain(n + 3)
-        scale(n + 2)
-        scale(n + 3)
-        shift_store(n + 2)
-        shift_store(n + 3)
+        for k in range(n, n + 3):
+            scale(k)
+        shift_store(n - 1)
         n += 4
-        for j in range(4):
-            residual(u - 1, j)
-            transpose_back(u - 1, j)
-            stats(n + j)
-            if j > 0:
-                centre_gain(n + j - 1)
-            aggregate(n + j)
-            if j % 2 == 1:
-                one_over_std(n + j - 1)
-            if j == 2:
-                scale(n)
-                shift_store(n)
-        centre_gain(n + 3)
+        aggregate(n)
+        residual(u - 1, 1)
+        transpose_back(u - 1, 1)
+        stats(n + 1)
+        centre_gain(n)
+        aggregate(n + 1)
+        one_over_std(n)
+        shift_store(n - 4)
+        residual(u - 1, 2)
+        transpose_back(u - 1, 2)
+        stats(n + 2)
+        centre_gain(n + 1)
+        aggregate(n + 2)
+        shift_store(n)
+        shift_store(n - 3)
+        residual(u - 1, 3)
+        transpose_back(u - 1, 3)
+        stats(n + 3)
+        centre_gain(n + 2)
+        aggregate(n + 3)
+        one_over_std(n + 2)
+        shift_store(n - 2)
         shift_store(n + 1)
+        centre_gain(n + 3)
+        shift_store(n - 1)
         shift_store(n + 2)
         shift_store(n + 3)

@@ -23,6 +23,7 @@ TILES = GROUP // P
 GROUPS = TOKENS // GROUP
 BANK = 512
 UNITS = (4, 4, 4, 4, 4, 4, 4, 4)
+LATE = (3, 11, 19,)
 START = [sum(UNITS[:u]) for u in range(len(UNITS) + 1)]
 
 
@@ -349,7 +350,8 @@ def tile_ffnn_encoder_pc_t_kernel(tc, h_attn, W1, b1, W2, b2, g2, beta2, out):
         def centre_gain(n):
             if outside(n):
                 return
-            t1 = work.tile([P, D], F32, tag="t1", name="t1", bufs=8)
+            tag, bufs = ("t1_late", len(LATE)) if n in LATE else ("t1", 8)
+            t1 = work.tile([P, D], F32, tag=tag, name=tag, bufs=bufs)
             live[("t1", n)] = t1
             nc.vector.scalar_tensor_tensor(
                 out=t1[:], in0=live[("xb", n)][:], scalar=live[("mv", n // 2)][:, n % 2, 0:1], in1=g2_bc[:],
@@ -359,7 +361,7 @@ def tile_ffnn_encoder_pc_t_kernel(tc, h_attn, W1, b1, W2, b2, g2, beta2, out):
         def one_over_std(n):
             if outside(n):
                 return
-            rstd = work.tile([P, 2], F32, tag="rstd", name="rstd", bufs=6)
+            rstd = work.tile([P, 2], F32, tag="rstd", name="rstd", bufs=16)
             live[("rstd", n // 2)] = rstd
             nc.scalar.activation(
                 out=rstd[:], in_=live[("mv", n // 2)][:, :, 1], func=ACT.Abs_reciprocal_sqrt,
@@ -444,12 +446,12 @@ def tile_ffnn_encoder_pc_t_kernel(tc, h_attn, W1, b1, W2, b2, g2, beta2, out):
         for b in range(4):
             second_matmul(0, b)
             bias_out(0, b)
-        nc.scalar.copy(out=beta2_sb[:], in_=beta2_bc[:])
         regroup_hidden(1, 0, "vector")
         residual(0, 0)
         for b in (4, 6):
             first_matmul(1, b)
             relu_out(1, b)
+        nc.vector.tensor_copy(out=beta2_sb[:], in_=beta2_bc[:])
         quantise_hidden(1, 0)
         regroup_hidden(1, 1)
         for u in range(2, len(UNITS)):
@@ -480,7 +482,8 @@ def tile_ffnn_encoder_pc_t_kernel(tc, h_attn, W1, b1, W2, b2, g2, beta2, out):
             quantise_h(u + 1)
             aggregate(n + 1)
             regroup_hidden(u, 0)
-            scale(n - 1)
+            if n - 1 in LATE:
+                scale(n - 1)
             shift_store(n - 3)
             centre_gain(n + 1)
             residual(u - 2, 2)
@@ -499,6 +502,8 @@ def tile_ffnn_encoder_pc_t_kernel(tc, h_attn, W1, b1, W2, b2, g2, beta2, out):
             stats(n + 3)
             quantise_hidden(u, 0)
             centre_gain(n + 2)
+            if n - 1 not in LATE:
+                shift_store(n - 1)
             one_over_std(n)
             for b in range(6 if u + 1 < len(UNITS) else 8, 8):
                 first_matmul(u, b)
@@ -520,7 +525,6 @@ def tile_ffnn_encoder_pc_t_kernel(tc, h_attn, W1, b1, W2, b2, g2, beta2, out):
         shift_store(n - 2)
         aggregate(n)
         shift_store(n - 4)
-        shift_store(7)
         centre_gain(n)
         stats(n + 1)
         residual(u - 2, 2)
@@ -535,7 +539,6 @@ def tile_ffnn_encoder_pc_t_kernel(tc, h_attn, W1, b1, W2, b2, g2, beta2, out):
         residual(u - 2, 3)
         transpose_back(u - 2, 3)
         stats(n + 2)
-        shift_store(15)
         aggregate(n + 2)
         stats(n + 3)
         centre_gain(n + 2)
@@ -549,7 +552,7 @@ def tile_ffnn_encoder_pc_t_kernel(tc, h_attn, W1, b1, W2, b2, g2, beta2, out):
         transpose_back(u - 1, 0)
         stats(n + 4)
         centre_gain(n + 3)
-        for k in range(n, n + 3):
+        for k in range(n, n + 4):
             scale(k)
         shift_store(n - 1)
         n += 4

@@ -310,7 +310,7 @@ def tile_ffnn_encoder_pc_t_kernel(tc, h_attn, W1, b1, W2, b2, g2, beta2, out):
 
         def residual(u, j):
             n = tile_of(u, j)
-            if n is None:
+            if n is None or ("xb", n) in live:
                 return
             xb = next_bank("v")
             live[("xb", n)] = xb
@@ -443,11 +443,12 @@ def tile_ffnn_encoder_pc_t_kernel(tc, h_attn, W1, b1, W2, b2, g2, beta2, out):
         copy_in(2, 0)
         copy_in(2, 1)
         quantise_h(2)
+        residual(0, 0)
         for b in range(4):
             second_matmul(0, b)
             bias_out(0, b)
+        residual(0, 1)
         regroup_hidden(1, 0, "vector")
-        residual(0, 0)
         for b in (4, 6):
             first_matmul(1, b)
             relu_out(1, b)
@@ -456,20 +457,20 @@ def tile_ffnn_encoder_pc_t_kernel(tc, h_attn, W1, b1, W2, b2, g2, beta2, out):
         regroup_hidden(1, 1)
         for u in range(2, len(UNITS)):
             n = 4 * (u - 2)
-            transpose_in(u + 1, 0)
-            transpose_back(u - 2, 0)
-            copy_in(u + 1, 0)
-            aggregate(n - 1)
-            stats(n)
-            centre_gain(n - 1)
             first_matmul(u, 0)
             relu_out(u, 0)
             first_matmul(u, 4)
             relu_out(u, 4)
-            residual(u - 2, 1)
-            transpose_back(u - 2, 1)
+            transpose_back(u - 2, 0)
+            aggregate(n - 1)
+            stats(n)
+            centre_gain(n - 1)
+            transpose_in(u + 1, 0)
+            copy_in(u + 1, 0)
             transpose_in(u + 1, 1)
             copy_in(u + 1, 1)
+            residual(u - 2, 1)
+            transpose_back(u - 2, 1)
             one_over_std(n - 2)
             aggregate(n)
             shift_store(n - 4)
@@ -487,8 +488,8 @@ def tile_ffnn_encoder_pc_t_kernel(tc, h_attn, W1, b1, W2, b2, g2, beta2, out):
             shift_store(n - 3)
             centre_gain(n + 1)
             residual(u - 2, 2)
-            transpose_back(u - 2, 2)
             residual(u - 2, 3)
+            transpose_back(u - 2, 2)
             transpose_back(u - 2, 3)
             stats(n + 2)
             shift_store(n - 2)

@@ -55,13 +55,14 @@ def tile_ffnn_encoder_pc_t_kernel(tc, h_attn, W1, b1, W2, b2, g2, beta2, out):
         nc.vector.memset(eps_t[:], EPS)
         ones = keep.tile([P, P], BF16)
         nc.vector.memset(ones[:], 1.0)
+        zeros = keep.tile([P, BANK], BF16)
+        nc.vector.memset(zeros[:], 0.0)
         ident = keep.tile([P, P], F32)
         make_identity(nc, ident[:])
         identb = keep.tile([P, P], BF16)
         make_identity(nc, identb[:])
 
         b1raw = keep.tile([P, 2, 4], BF16)
-        nc.scalar.dma_start(out=b1raw[:], in_=b1.rearrange("(g p t) -> p g t", g=2, t=4))
         nc.scalar.dma_start(out=b2rows[0:4, :], in_=b2.rearrange("(b p) -> b p", b=4))
         nc.scalar.dma_start(out=rows[0:1, 0:D], in_=g2.rearrange("(o d) -> o d", o=1))
         nc.scalar.dma_start(out=rows[0:1, D:2 * D], in_=beta2.rearrange("(o d) -> o d", o=1))
@@ -93,6 +94,7 @@ def tile_ffnn_encoder_pc_t_kernel(tc, h_attn, W1, b1, W2, b2, g2, beta2, out):
                 in_=h[0:GROUP, :].rearrange("(p j) d -> p (j d)", j=TILES)[:, pair * 2 * D:(pair + 1) * 2 * D],
             )
             load_w1(pair)
+        nc.sync.dma_start(out=b1raw[:], in_=b1.rearrange("(g p t) -> p g t", g=2, t=4))
         for half in range(2):
             nc.sync.dma_start(
                 out=w2raw[:, half],
@@ -107,6 +109,11 @@ def tile_ffnn_encoder_pc_t_kernel(tc, h_attn, W1, b1, W2, b2, g2, beta2, out):
         g2_bc = keep.tile([P, D], F32)
         beta2_sb = keep.tile([P, D], F32)
         b2f = keep.tile([P, 4], F32)
+
+        def keep_clock(count):
+            idle = next_bank("v")
+            for k in range(count):
+                nc.tensor.matmul(out=idle[:], lhsT=zeros[:, 0:P], rhs=zeros[:], start=True, stop=True)
 
         def spread_vectors():
             nc.tensor.matmul(out=beta2_bc[:], lhsT=ones[:], rhs=rows[:, D:2 * D], start=True, stop=True)
@@ -394,10 +401,12 @@ def tile_ffnn_encoder_pc_t_kernel(tc, h_attn, W1, b1, W2, b2, g2, beta2, out):
                 out=o[g * GROUP:(g + 1) * GROUP, :].rearrange("(p j) d -> p j d", j=TILES)[:, j, :], in_=ot[:],
             )
 
+        keep_clock(4)
         transpose_in(0, 0)
         copy_in(0, 0)
         spread_vectors()
         transpose_in(0, 1)
+        keep_clock(4)
         for s in range(4):
             regroup_w1(0, s, "vector" if s < 2 else "scalar")
         copy_in(0, 1)

from contextlib import ExitStack

import concourse.mybir as mybir
from concourse.masks import make_identity

F32 = mybir.dt.float32
BF16 = mybir.dt.bfloat16
U32 = mybir.dt.uint32
U8 = mybir.dt.uint8
FP8X4 = mybir.dt.float8_e4m3fn_x4
ALU = mybir.AluOpType
ACT = mybir.ActivationFunctionType

P = 128
TOKENS = 4096
D = 512
F = 1024
EPS = 1e-3
FLOPS = 2 * TOKENS * D * F * 2

GROUP = 512
TILES = GROUP // P
GROUPS = TOKENS // GROUP
BANK = 512
UNITS = (4, 4, 4, 4, 4, 4, 4, 4)
LATE = (3, 11, 19,)
START = [sum(UNITS[:u]) for u in range(len(UNITS) + 1)]


def tile_ffnn_encoder_pc_t_kernel(tc, h_attn, W1, b1, W2, b2, g2, beta2, out):
    nc = tc.nc
    h = h_attn.flatten_outer_dims()
    o = out.flatten_outer_dims()
    with ExitStack() as ctx:
        keep = ctx.enter_context(tc.tile_pool(name="keep", bufs=1))
        work = ctx.enter_context(tc.tile_pool(name="work", bufs=2))
        psum = ctx.enter_context(tc.psum_pool(name="psum", bufs=1))
        ctx.enter_context(tc.manual_schedule())

        ring_size = {"s": 4, "v": 3}
        ring_next = {"s": 0, "v": 0}

        def next_bank(ring, dtype=F32, cols=BANK):
            k = ring_next[ring] % ring_size[ring]
            ring_next[ring] += 1
            return psum.tile([P, cols], dtype, tag="%s%d" % (ring, k), name="%s%d" % (ring, k))

        live = {}

        rows = keep.tile([P, 2 * D], BF16)
        nc.vector.memset(rows[:], 0.0)
        b2rows = keep.tile([P, P], BF16)
        nc.vector.memset(b2rows[:], 0.0)
        eps_t = keep.tile([P, 1], F32)
        nc.vector.memset(eps_t[:], EPS)
        ones = keep.tile([P, P], BF16)
        nc.vector.memset(ones[:], 1.0)
        zeros = keep.tile([P, BANK], BF16)
        nc.vector.memset(zeros[:], 0.0)
        ident = keep.tile([P, P], F32)
        make_identity(nc, ident[:])
        identb = keep.tile([P, P], BF16)
        make_identity(nc, identb[:])

        b1raw = keep.tile([P, 2, 4], BF16)
        nc.scalar.dma_start(out=b2rows[0:4, :], in_=b2.rearrange("(b p) -> b p", b=4))
        nc.scalar.dma_start(out=rows[0:1, 0:D], in_=g2.rearrange("(o d) -> o d", o=1))
        nc.scalar.dma_start(out=rows[0:1, D:2 * D], in_=beta2.rearrange("(o d) -> o d", o=1))
        warm = keep.tile([P, 1], F32)
        nc.scalar.activation(out=warm[:], in_=eps_t[:], func=ACT.Abs_reciprocal_sqrt)

        h_sb = [keep.tile([P, TILES * D], BF16, name="h%d" % g) for g in range(GROUPS)]
        w1raw = [keep.tile([P, 4, F // 2], BF16, name="w1raw%d" % half) for half in range(2)]
        w2raw = keep.tile([P, 2, 4, D], BF16)

        def load_h(g):
            nc.sync.dma_start(
                out=h_sb[g][:],
                in_=h[g * GROUP:(g + 1) * GROUP, :].rearrange("(p j) d -> p (j d)", j=TILES),
            )

        def load_w1(half):
            for u in range(2):
                nc.sync.dma_start(
                    out=w1raw[half][:, 2 * u:2 * u + 2, :],
                    in_=W1[256 * u:256 * u + 256, half * 512:(half + 1) * 512].rearrange(
                        "(q e) f -> q e f", e=2
                    ),
                )

        for pair in range(2):
            nc.sync.dma_start(
                out=h_sb[0][:, pair * 2 * D:(pair + 1) * 2 * D],
                in_=h[0:GROUP, :].rearrange("(p j) d -> p (j d)", j=TILES)[:, pair * 2 * D:(pair + 1) * 2 * D],
            )
            load_w1(pair)
        nc.sync.dma_start(out=b1raw[:], in_=b1.rearrange("(g p t) -> p g t", g=2, t=4))
        for half in range(2):
            nc.sync.dma_start(
                out=w2raw[:, half],
                in_=W2[512 * half:512 * half + 512, :].rearrange("(p t) d -> p t d", t=4),
            )
            load_h(half + 1)
        for g in range(3, GROUPS):
            load_h(g)

        b1f = keep.tile([P, 8], F32)
        beta2_bc = psum.tile([P, D], BF16, tag="beta2", name="beta2_bc")
        g2_bc = keep.tile([P, D], F32)
        beta2_sb = keep.tile([P, D], F32)
        b2f = keep.tile([P, 4], F32)

        def keep_clock(count):
            idle = next_bank("v")
            for k in range(count):
                nc.tensor.matmul(out=idle[:], lhsT=zeros[:, 0:P], rhs=zeros[:], start=True, stop=True)

        def spread_vectors():
            nc.tensor.matmul(out=beta2_bc[:], lhsT=ones[:], rhs=rows[:, D:2 * D], start=True, stop=True)
            live["g2"] = next_bank("v")
            nc.tensor.matmul(out=live["g2"][:], lhsT=ones[:], rhs=rows[:, 0:D], start=True, stop=True)
            live["b2"] = next_bank("v", BF16, P)
            nc.tensor.transpose(live["b2"][:], b2rows[:], identb[:])

        def keep_vectors():
            nc.vector.tensor_copy(out=b1f[:], in_=b1raw[:].rearrange("p g t -> p (g t)"))
            nc.vector.tensor_copy(out=g2_bc[:], in_=live["g2"][:])
            nc.vector.tensor_copy(out=b2f[:], in_=live["b2"][:, 0:4])

        def regroup(engine, out, in_):
            if engine == "gpsimd":
                nc.gpsimd.tensor_scalar(out=out, in0=in_, scalar1=1.0, scalar2=0.0, op0=ALU.mult, op1=ALU.add)
            elif engine == "vector":
                nc.vector.tensor_copy(out=out, in_=in_)
            else:
                nc.scalar.copy(out=out, in_=in_)

        w1g = keep.tile([P, 4 * F], BF16, align_bytes=64)
        w1c = keep.tile([P, F], U32, align_bytes=64)
        w1s = keep.tile([P, F], U8, align_bytes=64)
        w2g = keep.tile([P, 2 * 4 * D], BF16, align_bytes=64)
        w2c = keep.tile([P, 2 * D], U32, align_bytes=64)
        w2s = keep.tile([P, 2 * D], U8, align_bytes=64)

        def regroup_w1(half, s, engine):
            block = 4 * half + s
            regroup(
                engine,
                w1g[:, block * 512:(block + 1) * 512].rearrange("q (p t) -> q p t", t=4),
                w1raw[half][:].rearrange("q t (p s) -> q s p t", s=4)[:, s],
            )

        def quantise_w1(half):
            nc.vector.quantize_mx(
                out=w1c[:, half * 512:(half + 1) * 512].bitcast(FP8X4),
                scales=w1s[:, half * 512:(half + 1) * 512],
                in_=w1g[:, half * 2048:(half + 1) * 2048],
            )

        def regroup_w2(half, quarter, engine):
            lo = quarter * 256
            regroup(
                engine,
                w2g[:, half * 2048 + 4 * lo:half * 2048 + 4 * lo + 1024].rearrange("p (c i t) -> p c t i", i=4, t=4),
                w2raw[:, half, :, lo:lo + 256].rearrange("p t (c i) -> p c t i", i=4),
            )

        def quantise_w2(half):
            nc.vector.quantize_mx(
                out=w2c[:, half * D:(half + 1) * D].bitcast(FP8X4),
                scales=w2s[:, half * D:(half + 1) * D],
                in_=w2g[:, half * 2048:(half + 1) * 2048],
            )


        def absent(u):
            return u < 0 or u >= len(UNITS)

        def tokens(u):
            return UNITS[u] * P

        def h_tile(n):
            return h_sb[n // TILES][:, (n % TILES) * D:(n % TILES + 1) * D]

        def transpose_in(u, pair):
            if absent(u) or 2 * pair >= UNITS[u]:
                return
            xt = next_bank("s")
            live[("xt", u, pair)] = xt
            for jl in range(2):
                words = h_tile(START[u] + 2 * pair + jl).bitcast(F32)
                for k in range(2):
                    nc.tensor.transpose(
                        xt[:, k * 256 + jl * 128:k * 256 + jl * 128 + 128],
                        words[:, k * 128:k * 128 + 128],
                        ident[:],
                    )

        def copy_in(u, pair):
            if absent(u) or 2 * pair >= UNITS[u]:
                return
            if pair == 0:
                live[("hg", u)] = work.tile([P, 4 * GROUP], BF16, align_bytes=64, tag="hg", name="hg", bufs=2)
            pairs = live[("hg", u)][:].bitcast(F32).rearrange("q (c k) -> q c k", k=2)
            nc.scalar.copy(
                out=pairs[:, pair * 256:(pair + 1) * 256, :],
                in_=live[("xt", u, pair)][:].rearrange("q (k c) -> q c k", k=2),
            )

        def quantise_h(u):
            if absent(u):
                return
            hc = work.tile([P, GROUP], U32, align_bytes=64, tag="hc", name="hc", bufs=3)
            hs = work.tile([P, GROUP], U8, align_bytes=64, tag="hs", name="hs", bufs=3)
            live[("hc", u)] = (hc, hs)
            c = tokens(u)
            nc.vector.quantize_mx(out=hc[:, 0:c].bitcast(FP8X4), scales=hs[:, 0:c], in_=live[("hg", u)][:, 0:4 * c])

        def first_matmul(u, b, ring="s"):
            if absent(u):
                return
            hc, hs = live[("hc", u)]
            hp = next_bank(ring)
            live[("hp", u, b)] = hp
            c = tokens(u)
            nc.tensor.matmul_mx(
                out=hp[:, 0:c],
                lhsT=w1c[:, b * 128:(b + 1) * 128].bitcast(FP8X4),
                lhsT_scale=w1s[:, b * 128:(b + 1) * 128],
                rhs=hc[:, 0:c].bitcast(FP8X4),
                rhs_scale=hs[:, 0:c],
                start=True,
                stop=True,
            )

        def relu_out(u, b, engine="scalar"):
            if absent(u):
                return
            if ("planes", u, b // 4) not in live:
                live[("planes", u, b // 4)] = work.tile([P, 4, GROUP], BF16, tag="planes", name="planes", bufs=4)
            c = tokens(u)
            out = live[("planes", u, b // 4)][:, b % 4, 0:c]
            if engine == "scalar":
                nc.scalar.activation(
                    out=out, in_=live[("hp", u, b)][:, 0:c], func=ACT.Relu, bias=b1f[:, b:b + 1], scale=1.0,
                )
            else:
                nc.vector.tensor_scalar(
                    out=out, in0=live[("hp", u, b)][:, 0:c], scalar1=b1f[:, b:b + 1], scalar2=0.0,
                    op0=ALU.add, op1=ALU.max,
                )

        def regroup_hidden(u, half, engine="gpsimd"):
            if absent(u):
                return
            tag, bufs = ("hid_v", 2) if engine == "vector" else ("hid_g", 1)
            hid_g = work.tile([P, 4 * GROUP], BF16, align_bytes=64, tag=tag, name=tag, bufs=bufs)
            live[("hid_g", u, half)] = hid_g
            planes = live[("planes", u, half)]
            c = tokens(u)
            cut = {"gpsimd": c, "both": c // 2}.get(engine, 0)
            if cut:
                regroup(
                    "gpsimd",
                    hid_g[:, 0:4 * cut].rearrange("p (c t) -> p c t", t=4),
                    planes[:, :, 0:cut].rearrange("p t c -> p c t"),
                )
            if cut < c:
                regroup(
                    "vector" if engine == "vector" else "scalar",
                    hid_g[:, 4 * cut:4 * c].rearrange("p (c i t) -> p c t i", i=4, t=4),
                    planes[:, :, cut:c].rearrange("p t (c i) -> p c t i", i=4),
                )

        def quantise_hidden(u, half):
            if absent(u):
                return
            hid_c = work.tile([P, GROUP], U32, align_bytes=64, tag="hid_c", name="hid_c", bufs=4)
            hid_s = work.tile([P, GROUP], U8, align_bytes=64, tag="hid_s", name="hid_s", bufs=4)
            live[("hid_c", u, half)] = (hid_c, hid_s)
            c = tokens(u)
            nc.vector.quantize_mx(
                out=hid_c[:, 0:c].bitcast(FP8X4), scales=hid_s[:, 0:c], in_=live[("hid_g", u, half)][:, 0:4 * c]
            )

        def second_matmul(u, b, ring="s"):
            if absent(u):
                return
            ft = next_bank(ring)
            live[("ft", u, b)] = ft
            c = tokens(u)
            for half in range(2):
                hid_c, hid_s = live[("hid_c", u, half)]
                nc.tensor.matmul_mx(
                    out=ft[:, 0:c],
                    lhsT=w2c[:, half * D + b * 128:half * D + (b + 1) * 128].bitcast(FP8X4),
                    lhsT_scale=w2s[:, half * D + b * 128:half * D + (b + 1) * 128],
                    rhs=hid_c[:, 0:c].bitcast(FP8X4),
                    rhs_scale=hid_s[:, 0:c],
                    start=(half == 0),
                    stop=(half == 1),
                )

        def bias_out(u, b):
            if absent(u):
                return
            if b == 0:
                live[("x_t", u)] = work.tile([P, 4, GROUP], F32, tag="x_t", name="x_t", bufs=2)
            c = tokens(u)
            nc.scalar.activation(
                out=live[("x_t", u)][:, b, 0:c], in_=live[("ft", u, b)][:, 0:c],
                func=ACT.Identity, bias=b2f[:, b:b + 1], scale=1.0,
            )

        def tile_of(u, j):
            return None if absent(u) or j >= UNITS[u] else START[u] + j

        def residual(u, j):
            n = tile_of(u, j)
            if n is None or ("xb", n) in live:
                return
            xb = next_bank("v")
            live[("xb", n)] = xb
            nc.tensor.matmul(out=xb[:], lhsT=identb[:], rhs=h_tile(n), start=True, stop=False)

        def transpose_back(u, j):
            n = tile_of(u, j)
            if n is None:
                return
            for b in range(4):
                nc.tensor.matmul(
                    out=live[("xb", n)][:, b * 128:(b + 1) * 128],
                    lhsT=live[("x_t", u)][:, b, j * 128:(j + 1) * 128],
                    rhs=ident[:],
                    is_transpose=True,
                    start=False,
                    stop=(b == 3),
                )

        def outside(n):
            return n is None or n < 0 or n >= START[-1]

        def stats(n):
            if outside(n):
                return
            st = work.tile([P, 6], F32, tag="st", name="st", bufs=6)
            live[("st", n)] = st
            nc.vector.bn_stats(out=st[:], in_=live[("xb", n)][:])

        def aggregate(n):
            if outside(n):
                return
            if n % 2 == 0:
                live[("mv", n // 2)] = work.tile([P, 2, 2], F32, tag="mv", name="mv", bufs=6)
            nc.vector.bn_aggr(out=live[("mv", n // 2)][:, n % 2, :], in_=live[("st", n)][:])

        def centre_gain(n):
            if outside(n):
                return
            tag, bufs = ("t1_late", len(LATE)) if n in LATE else ("t1", 8)
            t1 = work.tile([P, D], F32, tag=tag, name=tag, bufs=bufs)
            live[("t1", n)] = t1
            nc.vector.scalar_tensor_tensor(
                out=t1[:], in0=live[("xb", n)][:], scalar=live[("mv", n // 2)][:, n % 2, 0:1], in1=g2_bc[:],
                op0=ALU.subtract, op1=ALU.mult,
            )

        def one_over_std(n):
            if outside(n):
                return
            rstd = work.tile([P, 2], F32, tag="rstd", name="rstd", bufs=16)
            live[("rstd", n // 2)] = rstd
            nc.scalar.activation(
                out=rstd[:], in_=live[("mv", n // 2)][:, :, 1], func=ACT.Abs_reciprocal_sqrt,
                bias=eps_t[:, 0:1], scale=1.0,
            )

        def scale(n):
            if outside(n):
                return
            t2 = work.tile([P, D], F32, tag="t2", name="t2", bufs=11)
            live[("t2", n)] = t2
            nc.scalar.activation(
                out=t2[:], in_=live[("t1", n)][:], func=ACT.Copy, scale=live[("rstd", n // 2)][:, n % 2:n % 2 + 1],
            )

        def shift_store(n):
            if outside(n):
                return
            if ("t2", n) in live:
                ot = live[("t2", n)]
                nc.gpsimd.tensor_tensor(out=ot[:], in0=ot[:], in1=beta2_sb[:], op=ALU.add)
            else:
                ot = work.tile([P, D], F32, tag="ot", name="ot", bufs=6)
                nc.vector.scalar_tensor_tensor(
                    out=ot[:], in0=live[("t1", n)][:], scalar=live[("rstd", n // 2)][:, n % 2:n % 2 + 1],
                    in1=beta2_bc[:], op0=ALU.mult, op1=ALU.add,
                )
            g, j = divmod(n, TILES)
            nc.sync.dma_start(
                out=o[g * GROUP:(g + 1) * GROUP, :].rearrange("(p j) d -> p j d", j=TILES)[:, j, :], in_=ot[:],
            )

        keep_clock(4)
        transpose_in(0, 0)
        copy_in(0, 0)
        spread_vectors()
        transpose_in(0, 1)
        keep_clock(4)
        for s in range(4):
            regroup_w1(0, s, "vector" if s < 2 else "scalar")
        copy_in(0, 1)
        quantise_w1(0)
        quantise_h(0)
        for s in range(4):
            regroup_w1(1, s, "vector" if s < 2 else "scalar")
        keep_vectors()
        quantise_w1(1)
        for b in range(4):
            first_matmul(0, b, "sv"[b % 2])
        transpose_in(1, 0)
        transpose_in(1, 1)
        for b in range(4):
            relu_out(0, b, ("scalar", "vector")[b % 2])
        copy_in(1, 0)
        copy_in(1, 1)
        regroup_w2(1, 0, "gpsimd")
        for b in (7, 4, 5, 6):
            first_matmul(0, b, "v" if b == 7 else "s")
        relu_out(0, 7, "vector")
        for b in range(4, 7):
            relu_out(0, b)
        quantise_h(1)
        regroup_hidden(0, 0, "vector")
        regroup_w2(0, 0, "scalar")
        regroup_w2(0, 1, "scalar")
        regroup_hidden(0, 1, "vector")
        quantise_hidden(0, 0)
        regroup_w2(1, 1, "vector")
        quantise_hidden(0, 1)
        quantise_w2(1)
        quantise_w2(0)
        for b in range(4):
            first_matmul(1, b)
            relu_out(1, b)
        first_matmul(1, 5, "v")
        first_matmul(1, 7, "v")
        relu_out(1, 5, "vector")
        relu_out(1, 7, "vector")
        transpose_in(2, 0)
        transpose_in(2, 1)
        copy_in(2, 0)
        copy_in(2, 1)
        quantise_h(2)
        residual(0, 0)
        for b in range(4):
            second_matmul(0, b)
            bias_out(0, b)
        residual(0, 1)
        regroup_hidden(1, 0, "vector")
        for b in (4, 6):
            first_matmul(1, b)
            relu_out(1, b)
        nc.vector.tensor_copy(out=beta2_sb[:], in_=beta2_bc[:])
        quantise_hidden(1, 0)
        regroup_hidden(1, 1)
        for u in range(2, len(UNITS)):
            n = 4 * (u - 2)
            first_matmul(u, 0)
            relu_out(u, 0)
            first_matmul(u, 4)
            relu_out(u, 4)
            transpose_back(u - 2, 0)
            aggregate(n - 1)
            stats(n)
            centre_gain(n - 1)
            transpose_in(u + 1, 0)
            copy_in(u + 1, 0)
            transpose_in(u + 1, 1)
            copy_in(u + 1, 1)
            residual(u - 2, 1)
            transpose_back(u - 2, 1)
            one_over_std(n - 2)
            aggregate(n)
            shift_store(n - 4)
            centre_gain(n)
            stats(n + 1)
            for b in range(1, 4):
                first_matmul(u, b)
                relu_out(u, b)
            quantise_hidden(u - 1, 1)
            quantise_h(u + 1)
            aggregate(n + 1)
            regroup_hidden(u, 0)
            if n - 1 in LATE:
                scale(n - 1)
            shift_store(n - 3)
            centre_gain(n + 1)
            residual(u - 2, 2)
            residual(u - 2, 3)
            transpose_back(u - 2, 2)
            transpose_back(u - 2, 3)
            stats(n + 2)
            shift_store(n - 2)
            aggregate(n + 2)
            for b in range(5, 6 if u + 1 < len(UNITS) else 8):
                first_matmul(u, b)
                relu_out(u, b)
            for b in range(4):
                second_matmul(u - 1, b)
                bias_out(u - 1, b)
            stats(n + 3)
            quantise_hidden(u, 0)
            centre_gain(n + 2)
            if n - 1 not in LATE:
                shift_store(n - 1)
            one_over_std(n)
            for b in range(6 if u + 1 < len(UNITS) else 8, 8):
                first_matmul(u, b)
                relu_out(u, b)
            residual(u - 1, 0)
            regroup_hidden(u, 1, "gpsimd" if u + 1 < len(UNITS) else "both")
        u = len(UNITS)
        n = 4 * (u - 2)
        aggregate(n - 1)
        centre_gain(n - 1)
        residual(u - 2, 1)
        one_over_std(n - 2)
        transpose_back(u - 2, 0)
        stats(n)
        transpose_back(u - 2, 1)
        scale(n - 2)
        scale(n - 1)
        quantise_hidden(u - 1, 1)
        shift_store(n - 2)
        aggregate(n)
        shift_store(n - 4)
        centre_gain(n)
        stats(n + 1)
        residual(u - 2, 2)
        transpose_back(u - 2, 2)
        aggregate(n + 1)
        for b in range(4):
            second_matmul(u - 1, b)
            bias_out(u - 1, b)
        shift_store(n - 3)
        shift_store(11)
        centre_gain(n + 1)
        residual(u - 2, 3)
        transpose_back(u - 2, 3)
        stats(n + 2)
        aggregate(n + 2)
        stats(n + 3)
        centre_gain(n + 2)
        aggregate(n + 3)
        one_over_std(n)
        one_over_std(n + 2)
        for k in (19,):
            shift_store(k)
        shift_store(3)
        residual(u - 1, 0)
        transpose_back(u - 1, 0)
        stats(n + 4)
        centre_gain(n + 3)
        for k in range(n, n + 4):
            scale(k)
        shift_store(n - 1)
        n += 4
        aggregate(n)
        residual(u - 1, 1)
        transpose_back(u - 1, 1)
        stats(n + 1)
        centre_gain(n)
        aggregate(n + 1)
        one_over_std(n)
        shift_store(n - 4)
        residual(u - 1, 2)
        transpose_back(u - 1, 2)
        stats(n + 2)
        centre_gain(n + 1)
        aggregate(n + 2)
        shift_store(n)
        shift_store(n - 3)
        residual(u - 1, 3)
        transpose_back(u - 1, 3)
        stats(n + 3)
        centre_gain(n + 2)
        aggregate(n + 3)
        one_over_std(n + 2)
        shift_store(n - 2)
        shift_store(n + 1)
        centre_gain(n + 3)
        shift_store(n - 1)
        shift_store(n + 2)
        shift_store(n + 3)
